import numpy as np
import ml_dtypes

BF16 = ml_dtypes.bfloat16


def bf(x):
    return np.asarray(x, np.float32).astype(BF16)


def f32(x):
    return np.asarray(x, np.float32)


def f64(x):
    return np.asarray(x).astype(np.float64)


def striped(idx):
    return np.tile(idx.reshape(-1, 16).T, (8, 1))


C, S, N, K, HALF, COV, R, ES = 128, 1024, 8192, 16, 512, 512, 256, 128
UW = 0.3


def softplus(v):
    return np.log(1.0 + np.exp(v))


def setup_inputs():
    nrm = np.random.standard_normal
    return {
        "emb": f32(np.random.uniform(size=(C, S))),
        "cov": bf(nrm((COV, N))),
        "y_t": f32(nrm((1, N))),
        "y_0_hat": f32(nrm((1, N))),
        "wr1": bf(nrm((COV, R)) / np.sqrt(COV)),
        "br1": f32(0.2 * nrm((R, 1))),
        "wr2": bf(2.0 * nrm((R, ES)) / np.sqrt(R)),
        "br2": f32(0.3 * nrm((ES, 1))),
        "wc": bf(0.5 * nrm((COV, C)) / np.sqrt(COV)),
        "bc": f32(0.1 * nrm((C, 1))),
        "wa": bf(2.0 * nrm((ES, C))),
        "wb": bf(2.0 * nrm((ES, C))),
        "wd": bf(nrm((ES, C))),
        "ua": f32(2.0 * nrm((C, 1))),
        "ub": f32(2.0 * nrm((C, 1))),
        "ud": f32(nrm((C, 1))),
        "offs": striped(np.concatenate([np.random.permutation(S)[:HALF] for _ in range(K)])),
    }


def reference(emb, cov, y_t, y_0_hat, wr1, br1, wr2, br2, wc, bc, wa, wb, wd, ua, ub, ud, offs):
    idx = offs[:16].T.reshape(-1)
    cv = f64(cov)
    hid = np.maximum(f64(wr1).T @ cv + f64(br1), 0.0)
    z = f64(wr2).T @ hid + f64(br2)
    ez = np.exp(z)
    p = (1.0 - UW) * ez / ez.sum(axis=0, keepdims=True)
    mod = f64(wc).T @ cv + f64(bc)
    ma = UW * f64(ua) + f64(wa).T @ p
    mb = UW * f64(ub) + f64(wb).T @ p
    md = UW * f64(ud) + f64(wd).T @ p
    mix = ma * f64(y_t) + mb * f64(y_0_hat) + md
    q = f64(emb)[:, idx] * mix
    return softplus(q * (1.0 + mod))

@@ -1,0 +1,178 @@
+import math
+
+import concourse.mybir as mybir
+
+F32 = mybir.dt.float32
+BF16 = mybir.dt.bfloat16
+U16 = mybir.dt.uint16
+ALU = mybir.AluOpType
+ACT = mybir.ActivationFunctionType
+
+P = 128
+STEPS = 1024
+N = 8192
+COV = 512
+HID = 256
+KC = COV // P
+KH = HID // P
+T = 512
+LOAD = 1024
+SPECIAL = 0.7
+UNIVERSAL = 0.3
+CLAMP = 30.0
+
+FLOPS = 2 * N * (COV * HID + HID * P + COV * P + 3 * P * P)
+
+
+def tile_conditionalvelocitymodel_b_kernel(
+    tc, emb, cov, y_t, y_0_hat, wr1, br1, wr2, br2, wc, bc, wa, wb, wd, ua, ub, ud, offs, out
+):
+    nc = tc.nc
+    with (
+        tc.tile_pool(name="held", bufs=1) as held,
+        tc.tile_pool(name="loads", bufs=3) as loads,
+        tc.tile_pool(name="work", bufs=3) as work,
+        tc.psum_pool(name="psum_hid", bufs=2) as psum_hid,
+        tc.psum_pool(name="psum_one", bufs=1) as psum_one,
+    ):
+        offsets = held.tile([P, N // 16], U16, name="offsets")
+        nc.sync.dma_start(offsets[:], offs)
+
+        wr1_sb = held.tile([P, KC, HID], BF16, name="wr1_sb")
+        nc.sync.dma_start(wr1_sb[:], wr1.rearrange("(k p) m -> p k m", p=P))
+        wr2_sb = held.tile([P, KH, P], BF16, name="wr2_sb")
+        nc.sync.dma_start(wr2_sb[:], wr2.rearrange("(k p) m -> p k m", p=P))
+        wc_sb = held.tile([P, KC, P], BF16, name="wc_sb")
+        nc.sync.dma_start(wc_sb[:], wc.rearrange("(k p) m -> p k m", p=P))
+        wa_sb = held.tile([P, P], BF16, name="wa_sb")
+        nc.sync.dma_start(wa_sb[:], wa)
+        wb_sb = held.tile([P, P], BF16, name="wb_sb")
+        nc.sync.dma_start(wb_sb[:], wb)
+        wd_sb = held.tile([P, P], BF16, name="wd_sb")
+        nc.sync.dma_start(wd_sb[:], wd)
+        emb_sb = held.tile([P, STEPS], F32, name="emb_sb")
+        nc.sync.dma_start(emb_sb[:], emb)
+
+        br1_sb = [held.tile([P, 1], F32, name=f"br1_sb{h}") for h in range(KH)]
+        for h in range(KH):
+            nc.scalar.dma_start(br1_sb[h][:], br1[h * P : (h + 1) * P, :])
+        br2_sb = held.tile([P, 1], F32, name="br2_sb")
+        nc.scalar.dma_start(br2_sb[:], br2)
+        bc_sb = held.tile([P, 1], F32, name="bc_sb")
+        nc.scalar.dma_start(bc_sb[:], bc)
+        ua_sb = held.tile([P, 1], F32, name="ua_sb")
+        nc.scalar.dma_start(ua_sb[:], ua)
+        ub_sb = held.tile([P, 1], F32, name="ub_sb")
+        nc.scalar.dma_start(ub_sb[:], ub)
+        ud_sb = held.tile([P, 1], F32, name="ud_sb")
+        nc.scalar.dma_start(ud_sb[:], ud)
+
+        ua_share = held.tile([P, 1], F32, name="ua_share")
+        nc.vector.tensor_scalar_mul(ua_share[:], ua_sb[:], UNIVERSAL)
+        ub_share = held.tile([P, 1], F32, name="ub_share")
+        nc.vector.tensor_scalar_mul(ub_share[:], ub_sb[:], UNIVERSAL)
+        ud_share = held.tile([P, 1], F32, name="ud_share")
+        nc.vector.tensor_scalar_mul(ud_share[:], ud_sb[:], UNIVERSAL)
+        bc_plus_1 = held.tile([P, 1], F32, name="bc_plus_1")
+        nc.vector.tensor_scalar_add(bc_plus_1[:], bc_sb[:], 1.0)
+        br2_scaled = held.tile([P, 1], F32, name="br2_scaled")
+        nc.vector.tensor_scalar_add(br2_scaled[:], br2_sb[:], math.log(SPECIAL))
+        one_col = held.tile([P, 1], F32, name="one_col")
+        nc.vector.memset(one_col[:], 1.0)
+
+        ones = held.tile([P, P], BF16, name="ones")
+        nc.vector.memset(ones[:], 1.0)
+
+        cov_blocks = cov.rearrange("(k p) n -> p k n", p=P)
+
+        for first in range(0, N, LOAD):
+            cov_sb = loads.tile([P, KC, LOAD], BF16, name="cov_sb")
+            nc.sync.dma_start(cov_sb[:], cov_blocks[:, :, first : first + LOAD])
+            yt_sb = loads.tile([P, LOAD], F32, name="yt_sb")
+            nc.sync.dma_start(yt_sb[:], y_t[:, first : first + LOAD].broadcast_to([P, LOAD]))
+            y0_sb = loads.tile([P, LOAD], F32, name="y0_sb")
+            nc.sync.dma_start(y0_sb[:], y_0_hat[:, first : first + LOAD].broadcast_to([P, LOAD]))
+
+            for lo in range(0, LOAD, T):
+                j0 = first + lo
+
+                hid_sb = work.tile([P, KH, T], BF16, name="hid_sb")
+                for h in range(KH):
+                    hid_ps = psum_hid.tile([P, T], F32, name="hid_ps")
+                    for k in range(KC):
+                        nc.tensor.matmul(
+                            hid_ps[:],
+                            wr1_sb[:, k, h * P : (h + 1) * P],
+                            cov_sb[:, k, lo : lo + T],
+                            start=(k == 0),
+                            stop=(k == KC - 1),
+                        )
+                    nc.scalar.activation(hid_sb[:, h, :], hid_ps[:], ACT.Relu, bias=br1_sb[h][:])
+
+                z_ps = psum_one.tile([P, T], F32, name="z_ps")
+                for h in range(KH):
+                    nc.tensor.matmul(
+                        z_ps[:], wr2_sb[:, h, :], hid_sb[:, h, :], start=(h == 0), stop=(h == KH - 1)
+                    )
+
+                expz = work.tile([P, T], BF16, name="expz")
+                nc.scalar.activation(expz[:], z_ps[:], ACT.Exp, bias=br2_sb[:])
+                sum_ps = psum_one.tile([P, T], F32, name="sum_ps")
+                nc.tensor.matmul(sum_ps[:], ones[:], expz[:], start=True, stop=True)
+                log_sum = work.tile([P, T], F32, name="log_sum")
+                nc.scalar.activation(log_sum[:], sum_ps[:], ACT.Ln)
+                z_norm = work.tile([P, T], F32, name="z_norm")
+                nc.vector.scalar_tensor_tensor(
+                    z_norm[:], z_ps[:], br2_scaled[:], log_sum[:], ALU.add, ALU.subtract
+                )
+                p_sb = work.tile([P, T], BF16, name="p_sb")
+                nc.scalar.activation(p_sb[:], z_norm[:], ACT.Exp)
+
+                a_ps = psum_one.tile([P, T], F32, name="a_ps")
+                nc.tensor.matmul(a_ps[:], wa_sb[:], p_sb[:], start=True, stop=True)
+                b_ps = psum_one.tile([P, T], F32, name="b_ps")
+                nc.tensor.matmul(b_ps[:], wb_sb[:], p_sb[:], start=True, stop=True)
+                d_ps = psum_one.tile([P, T], F32, name="d_ps")
+                nc.tensor.matmul(d_ps[:], wd_sb[:], p_sb[:], start=True, stop=True)
+                ma_yt = work.tile([P, T], F32, name="ma_yt")
+                nc.vector.scalar_tensor_tensor(
+                    ma_yt[:], a_ps[:], ua_share[:], yt_sb[:, lo : lo + T], ALU.add, ALU.mult
+                )
+                mb_y0 = work.tile([P, T], F32, name="mb_y0")
+                nc.vector.scalar_tensor_tensor(
+                    mb_y0[:], b_ps[:], ub_share[:], y0_sb[:, lo : lo + T], ALU.add, ALU.mult
+                )
+                md_more = work.tile([P, T], F32, name="md_more")
+                nc.vector.scalar_tensor_tensor(
+                    md_more[:], d_ps[:], ud_share[:], ma_yt[:], ALU.add, ALU.add
+                )
+                mix = work.tile([P, T], F32, name="mix")
+                nc.gpsimd.tensor_tensor(mix[:], md_more[:], mb_y0[:], ALU.add)
+
+                picked = emb_sb[:].indirect(offsets[:, j0 // 16 : (j0 + T) // 16])
+                q = work.tile([P, T], F32, name="q")
+                nc.vector.tensor_tensor(q[:], picked, mix[:], ALU.mult)
+
+                mod_ps = psum_one.tile([P, T], F32, name="mod_ps")
+                for k in range(KC):
+                    nc.tensor.matmul(
+                        mod_ps[:],
+                        wc_sb[:, k, :],
+                        cov_sb[:, k, lo : lo + T],
+                        start=(k == 0),
+                        stop=(k == KC - 1),
+                    )
+                v = work.tile([P, T], F32, name="v")
+                nc.vector.scalar_tensor_tensor(
+                    v[:], mod_ps[:], bc_plus_1[:], q[:], ALU.add, ALU.mult
+                )
+
+                v_low = work.tile([P, T], F32, name="v_low")
+                nc.gpsimd.tensor_scalar_min(v_low[:], v[:], CLAMP)
+                exp_v = work.tile([P, T], F32, name="exp_v")
+                nc.scalar.activation(exp_v[:], v_low[:], ACT.Exp)
+                log_v = work.tile([P, T], F32, name="log_v")
+                nc.scalar.activation(log_v[:], exp_v[:], ACT.Ln, bias=one_col[:])
+                result = work.tile([P, T], F32, name="result")
+                nc.vector.tensor_tensor(result[:], v[:], log_v[:], ALU.max)
+                nc.sync.dma_start(out[:, j0 : j0 + T], result[:])

@@ -16,7 +16,8 @@ HID = 256
 KC = COV // P
 KH = HID // P
 T = 512
-LOAD = 1024
+CHUNK = 2048
+SPREAD = CHUNK // P
 SPECIAL = 0.7
 UNIVERSAL = 0.3
 CLAMP = 30.0
@@ -28,44 +29,41 @@ def tile_conditionalvelocitymodel_b_kernel(
     tc, emb, cov, y_t, y_0_hat, wr1, br1, wr2, br2, wc, bc, wa, wb, wd, ua, ub, ud, offs, out
 ):
     nc = tc.nc
+    cov_blocks = cov.rearrange("(k p) n -> p k n", p=P)
     with (
         tc.tile_pool(name="held", bufs=1) as held,
-        tc.tile_pool(name="loads", bufs=3) as loads,
+        tc.tile_pool(name="cov_pool", bufs=3) as cov_pool,
+        tc.tile_pool(name="chunks", bufs=2) as chunks,
         tc.tile_pool(name="work", bufs=3) as work,
         tc.psum_pool(name="psum_hid", bufs=2) as psum_hid,
         tc.psum_pool(name="psum_one", bufs=1) as psum_one,
     ):
-        offsets = held.tile([P, N // 16], U16, name="offsets")
-        nc.sync.dma_start(offsets[:], offs)
-
         wr1_sb = held.tile([P, KC, HID], BF16, name="wr1_sb")
         nc.sync.dma_start(wr1_sb[:], wr1.rearrange("(k p) m -> p k m", p=P))
-        wr2_sb = held.tile([P, KH, P], BF16, name="wr2_sb")
-        nc.sync.dma_start(wr2_sb[:], wr2.rearrange("(k p) m -> p k m", p=P))
-        wc_sb = held.tile([P, KC, P], BF16, name="wc_sb")
-        nc.sync.dma_start(wc_sb[:], wc.rearrange("(k p) m -> p k m", p=P))
-        wa_sb = held.tile([P, P], BF16, name="wa_sb")
-        nc.sync.dma_start(wa_sb[:], wa)
-        wb_sb = held.tile([P, P], BF16, name="wb_sb")
-        nc.sync.dma_start(wb_sb[:], wb)
-        wd_sb = held.tile([P, P], BF16, name="wd_sb")
-        nc.sync.dma_start(wd_sb[:], wd)
-        emb_sb = held.tile([P, STEPS], F32, name="emb_sb")
-        nc.sync.dma_start(emb_sb[:], emb)
 
         br1_sb = [held.tile([P, 1], F32, name=f"br1_sb{h}") for h in range(KH)]
         for h in range(KH):
             nc.scalar.dma_start(br1_sb[h][:], br1[h * P : (h + 1) * P, :])
+        wr2_sb = held.tile([P, KH, P], BF16, name="wr2_sb")
+        nc.scalar.dma_start(wr2_sb[:], wr2.rearrange("(k p) m -> p k m", p=P))
         br2_sb = held.tile([P, 1], F32, name="br2_sb")
         nc.scalar.dma_start(br2_sb[:], br2)
-        bc_sb = held.tile([P, 1], F32, name="bc_sb")
-        nc.scalar.dma_start(bc_sb[:], bc)
+        wa_sb = held.tile([P, P], BF16, name="wa_sb")
+        nc.scalar.dma_start(wa_sb[:], wa)
+        wb_sb = held.tile([P, P], BF16, name="wb_sb")
+        nc.scalar.dma_start(wb_sb[:], wb)
+        wd_sb = held.tile([P, P], BF16, name="wd_sb")
+        nc.scalar.dma_start(wd_sb[:], wd)
+        wc_sb = held.tile([P, KC, P], BF16, name="wc_sb")
+        nc.scalar.dma_start(wc_sb[:], wc.rearrange("(k p) m -> p k m", p=P))
         ua_sb = held.tile([P, 1], F32, name="ua_sb")
         nc.scalar.dma_start(ua_sb[:], ua)
         ub_sb = held.tile([P, 1], F32, name="ub_sb")
         nc.scalar.dma_start(ub_sb[:], ub)
         ud_sb = held.tile([P, 1], F32, name="ud_sb")
         nc.scalar.dma_start(ud_sb[:], ud)
+        bc_sb = held.tile([P, 1], F32, name="bc_sb")
+        nc.scalar.dma_start(bc_sb[:], bc)
 
         ua_share = held.tile([P, 1], F32, name="ua_share")
         nc.vector.tensor_scalar_mul(ua_share[:], ua_sb[:], UNIVERSAL)
@@ -79,23 +77,19 @@ def tile_conditionalvelocitymodel_b_kernel(
         nc.vector.tensor_scalar_add(br2_scaled[:], br2_sb[:], math.log(SPECIAL))
         one_col = held.tile([P, 1], F32, name="one_col")
         nc.vector.memset(one_col[:], 1.0)
+        ones_bf = held.tile([P, 1], BF16, name="ones_bf")
+        nc.vector.memset(ones_bf[:], 1.0)
 
-        ones = held.tile([P, P], BF16, name="ones")
-        nc.vector.memset(ones[:], 1.0)
-
-        cov_blocks = cov.rearrange("(k p) n -> p k n", p=P)
-
-        for first in range(0, N, LOAD):
-            cov_sb = loads.tile([P, KC, LOAD], BF16, name="cov_sb")
-            nc.sync.dma_start(cov_sb[:], cov_blocks[:, :, first : first + LOAD])
-            yt_sb = loads.tile([P, LOAD], F32, name="yt_sb")
-            nc.sync.dma_start(yt_sb[:], y_t[:, first : first + LOAD].broadcast_to([P, LOAD]))
-            y0_sb = loads.tile([P, LOAD], F32, name="y0_sb")
-            nc.sync.dma_start(y0_sb[:], y_0_hat[:, first : first + LOAD].broadcast_to([P, LOAD]))
-
-            for lo in range(0, LOAD, T):
-                j0 = first + lo
-
+        def router(c):
+            first = c * CHUNK
+            cov_sb = cov_pool.tile([P, KC, CHUNK], BF16, name="cov_sb")
+            for lo in range(0, CHUNK, T):
+                nc.sync.dma_start(
+                    cov_sb[:, :, lo : lo + T], cov_blocks[:, :, first + lo : first + lo + T]
+                )
+            exp_z = chunks.tile([P, CHUNK], BF16, name="exp_z")
+            exp_z_07 = chunks.tile([P, CHUNK], F32, name="exp_z_07")
+            for lo in range(0, CHUNK, T):
                 hid_sb = work.tile([P, KH, T], BF16, name="hid_sb")
                 for h in range(KH):
                     hid_ps = psum_hid.tile([P, T], F32, name="hid_ps")
@@ -108,26 +102,42 @@ def tile_conditionalvelocitymodel_b_kernel(
                             stop=(k == KC - 1),
                         )
                     nc.scalar.activation(hid_sb[:, h, :], hid_ps[:], ACT.Relu, bias=br1_sb[h][:])
-
                 z_ps = psum_one.tile([P, T], F32, name="z_ps")
                 for h in range(KH):
                     nc.tensor.matmul(
                         z_ps[:], wr2_sb[:, h, :], hid_sb[:, h, :], start=(h == 0), stop=(h == KH - 1)
                     )
+                nc.scalar.activation(exp_z[:, lo : lo + T], z_ps[:], ACT.Exp, bias=br2_sb[:])
+                nc.scalar.activation(exp_z_07[:, lo : lo + T], z_ps[:], ACT.Exp, bias=br2_scaled[:])
 
-                expz = work.tile([P, T], BF16, name="expz")
-                nc.scalar.activation(expz[:], z_ps[:], ACT.Exp, bias=br2_sb[:])
-                sum_ps = psum_one.tile([P, T], F32, name="sum_ps")
-                nc.tensor.matmul(sum_ps[:], ones[:], expz[:], start=True, stop=True)
-                log_sum = work.tile([P, T], F32, name="log_sum")
-                nc.scalar.activation(log_sum[:], sum_ps[:], ACT.Ln)
-                z_norm = work.tile([P, T], F32, name="z_norm")
-                nc.vector.scalar_tensor_tensor(
-                    z_norm[:], z_ps[:], br2_scaled[:], log_sum[:], ALU.add, ALU.subtract
+            sums_ps = psum_one.tile([P, SPREAD], F32, name="sums_ps")
+            every_spread = exp_z[:].rearrange("e (m b) -> e b m", b=SPREAD)
+            for b in range(SPREAD):
+                nc.tensor.matmul(
+                    sums_ps[:, b : b + 1], every_spread[:, b, :], ones_bf[:], start=True, stop=True
                 )
-                p_sb = work.tile([P, T], BF16, name="p_sb")
-                nc.scalar.activation(p_sb[:], z_norm[:], ACT.Exp)
+            inv_sum = chunks.tile([P, SPREAD], F32, name="inv_sum")
+            nc.vector.reciprocal(inv_sum[:], sums_ps[:])
+            parked = out[0:1, first : first + CHUNK]
+            nc.sync.dma_start(parked.rearrange("o (m b) -> (o m) b", b=SPREAD), inv_sum[:])
+            inv_rows = chunks.tile([P, CHUNK], F32, name="inv_rows")
+            nc.sync.dma_start(inv_rows[:], parked.broadcast_to([P, CHUNK]))
+            yt_sb = chunks.tile([P, CHUNK], F32, name="yt_sb")
+            nc.sync.dma_start(yt_sb[:], y_t[:, first : first + CHUNK].broadcast_to([P, CHUNK]))
+            y0_sb = chunks.tile([P, CHUNK], F32, name="y0_sb")
+            nc.sync.dma_start(y0_sb[:], y_0_hat[:, first : first + CHUNK].broadcast_to([P, CHUNK]))
+            return cov_sb, exp_z_07, inv_rows, yt_sb, y0_sb
 
+        def experts(c, cov_sb, exp_z_07, inv_rows, yt_sb, y0_sb):
+            first = c * CHUNK
+            v = chunks.tile([P, CHUNK], F32, name="v")
+            soft = chunks.tile([P, CHUNK], F32, name="soft")
+            for lo in range(0, CHUNK, T):
+                j0 = first + lo
+                p_sb = work.tile([P, T], BF16, name="p_sb")
+                nc.vector.tensor_tensor(
+                    p_sb[:], exp_z_07[:, lo : lo + T], inv_rows[:, lo : lo + T], ALU.mult
+                )
                 a_ps = psum_one.tile([P, T], F32, name="a_ps")
                 nc.tensor.matmul(a_ps[:], wa_sb[:], p_sb[:], start=True, stop=True)
                 b_ps = psum_one.tile([P, T], F32, name="b_ps")
@@ -162,17 +172,26 @@ def tile_conditionalvelocitymodel_b_kernel(
                         start=(k == 0),
                         stop=(k == KC - 1),
                     )
-                v = work.tile([P, T], F32, name="v")
                 nc.vector.scalar_tensor_tensor(
-                    v[:], mod_ps[:], bc_plus_1[:], q[:], ALU.add, ALU.mult
+                    v[:, lo : lo + T], mod_ps[:], bc_plus_1[:], q[:], ALU.add, ALU.mult
                 )
+                nc.gpsimd.tensor_scalar(
+                    soft[:, lo : lo + T], v[:, lo : lo + T], CLAMP, -CLAMP, ALU.min, ALU.max
+                )
+                nc.scalar.activation(soft[:, lo : lo + T], soft[:, lo : lo + T], ACT.Exp)
+            nc.scalar.activation(soft[:], soft[:], ACT.Ln, bias=one_col[:])
+            for lo in range(0, CHUNK, T):
+                nc.vector.tensor_tensor(
+                    soft[:, lo : lo + T], v[:, lo : lo + T], soft[:, lo : lo + T], ALU.max
+                )
+                nc.sync.dma_start(out[:, first + lo : first + lo + T], soft[:, lo : lo + T])
 
-                v_low = work.tile([P, T], F32, name="v_low")
-                nc.gpsimd.tensor_scalar_min(v_low[:], v[:], CLAMP)
-                exp_v = work.tile([P, T], F32, name="exp_v")
-                nc.scalar.activation(exp_v[:], v_low[:], ACT.Exp)
-                log_v = work.tile([P, T], F32, name="log_v")
-                nc.scalar.activation(log_v[:], exp_v[:], ACT.Ln, bias=one_col[:])
-                result = work.tile([P, T], F32, name="result")
-                nc.vector.tensor_tensor(result[:], v[:], log_v[:], ALU.max)
-                nc.sync.dma_start(out[:, j0 : j0 + T], result[:])
+        routed = router(0)
+        offsets = held.tile([P, N // 16], U16, name="offsets")
+        nc.sync.dma_start(offsets[:], offs)
+        emb_sb = held.tile([P, STEPS], F32, name="emb_sb")
+        nc.sync.dma_start(emb_sb[:], emb)
+        for c in range(N // CHUNK):
+            ahead = router(c + 1) if c + 1 < N // CHUNK else None
+            experts(c, *routed)
+            routed = ahead

@@ -16,11 +16,12 @@ HID = 256
 KC = COV // P
 KH = HID // P
 T = 512
-CHUNK = 2048
-SPREAD = CHUNK // P
+G = 1024
+GROUPS = N // G
+SPREAD = G // P
+BATCH = 2
 SPECIAL = 0.7
 UNIVERSAL = 0.3
-CLAMP = 30.0
 
 FLOPS = 2 * N * (COV * HID + HID * P + COV * P + 3 * P * P)
 
@@ -32,9 +33,9 @@ def tile_conditionalvelocitymodel_b_kernel(
     cov_blocks = cov.rearrange("(k p) n -> p k n", p=P)
     with (
         tc.tile_pool(name="held", bufs=1) as held,
-        tc.tile_pool(name="cov_pool", bufs=3) as cov_pool,
-        tc.tile_pool(name="chunks", bufs=2) as chunks,
+        tc.tile_pool(name="handed", bufs=3) as handed,
         tc.tile_pool(name="work", bufs=3) as work,
+        tc.tile_pool(name="batches", bufs=2) as batches,
         tc.psum_pool(name="psum_hid", bufs=2) as psum_hid,
         tc.psum_pool(name="psum_one", bufs=1) as psum_one,
     ):
@@ -80,16 +81,13 @@ def tile_conditionalvelocitymodel_b_kernel(
         ones_bf = held.tile([P, 1], BF16, name="ones_bf")
         nc.vector.memset(ones_bf[:], 1.0)
 
-        def router(c):
-            first = c * CHUNK
-            cov_sb = cov_pool.tile([P, KC, CHUNK], BF16, name="cov_sb")
-            for lo in range(0, CHUNK, T):
-                nc.sync.dma_start(
-                    cov_sb[:, :, lo : lo + T], cov_blocks[:, :, first + lo : first + lo + T]
-                )
-            exp_z = chunks.tile([P, CHUNK], BF16, name="exp_z")
-            exp_z_07 = chunks.tile([P, CHUNK], F32, name="exp_z_07")
-            for lo in range(0, CHUNK, T):
+        def router(g):
+            j0 = g * G
+            cov_sb = handed.tile([P, KC, G], BF16, name="cov_sb")
+            exp_z = work.tile([P, G], BF16, name="exp_z")
+            exp_z_07 = handed.tile([P, G], F32, name="exp_z_07")
+            for lo in range(0, G, T):
+                nc.sync.dma_start(cov_sb[:, :, lo : lo + T], cov_blocks[:, :, j0 + lo : j0 + lo + T])
                 hid_sb = work.tile([P, KH, T], BF16, name="hid_sb")
                 for h in range(KH):
                     hid_ps = psum_hid.tile([P, T], F32, name="hid_ps")
@@ -116,53 +114,50 @@ def tile_conditionalvelocitymodel_b_kernel(
                 nc.tensor.matmul(
                     sums_ps[:, b : b + 1], every_spread[:, b, :], ones_bf[:], start=True, stop=True
                 )
-            inv_sum = chunks.tile([P, SPREAD], F32, name="inv_sum")
+            inv_sum = work.tile([P, SPREAD], F32, name="inv_sum")
             nc.vector.reciprocal(inv_sum[:], sums_ps[:])
-            parked = out[0:1, first : first + CHUNK]
+            parked = out[0:1, j0 : j0 + G]
             nc.sync.dma_start(parked.rearrange("o (m b) -> (o m) b", b=SPREAD), inv_sum[:])
-            inv_rows = chunks.tile([P, CHUNK], F32, name="inv_rows")
-            nc.sync.dma_start(inv_rows[:], parked.broadcast_to([P, CHUNK]))
-            yt_sb = chunks.tile([P, CHUNK], F32, name="yt_sb")
-            nc.sync.dma_start(yt_sb[:], y_t[:, first : first + CHUNK].broadcast_to([P, CHUNK]))
-            y0_sb = chunks.tile([P, CHUNK], F32, name="y0_sb")
-            nc.sync.dma_start(y0_sb[:], y_0_hat[:, first : first + CHUNK].broadcast_to([P, CHUNK]))
-            return cov_sb, exp_z_07, inv_rows, yt_sb, y0_sb
+            inv_rows = handed.tile([P, G], F32, name="inv_rows")
+            nc.sync.dma_start(inv_rows[:], parked.broadcast_to([P, G]))
+            return cov_sb, exp_z_07, inv_rows
 
-        def experts(c, cov_sb, exp_z_07, inv_rows, yt_sb, y0_sb):
-            first = c * CHUNK
-            v = chunks.tile([P, CHUNK], F32, name="v")
-            soft = chunks.tile([P, CHUNK], F32, name="soft")
-            for lo in range(0, CHUNK, T):
-                j0 = first + lo
-                p_sb = work.tile([P, T], BF16, name="p_sb")
-                nc.vector.tensor_tensor(
-                    p_sb[:], exp_z_07[:, lo : lo + T], inv_rows[:, lo : lo + T], ALU.mult
-                )
+        def experts(g, cov_sb, exp_z_07, inv_rows, v, soft):
+            j0 = g * G
+            yt_sb = work.tile([P, G], F32, name="yt_sb")
+            nc.sync.dma_start(yt_sb[:], y_t[:, j0 : j0 + G].broadcast_to([P, G]))
+            y0_sb = work.tile([P, G], F32, name="y0_sb")
+            nc.sync.dma_start(y0_sb[:], y_0_hat[:, j0 : j0 + G].broadcast_to([P, G]))
+
+            p_sb = work.tile([P, G], BF16, name="p_sb")
+            nc.vector.tensor_tensor(p_sb[:], exp_z_07[:], inv_rows[:], ALU.mult)
+            mb_y0 = work.tile([P, G], F32, name="mb_y0")
+            md_more = work.tile([P, G], F32, name="md_more")
+            for lo in range(0, G, T):
                 a_ps = psum_one.tile([P, T], F32, name="a_ps")
-                nc.tensor.matmul(a_ps[:], wa_sb[:], p_sb[:], start=True, stop=True)
+                nc.tensor.matmul(a_ps[:], wa_sb[:], p_sb[:, lo : lo + T], start=True, stop=True)
                 b_ps = psum_one.tile([P, T], F32, name="b_ps")
-                nc.tensor.matmul(b_ps[:], wb_sb[:], p_sb[:], start=True, stop=True)
+                nc.tensor.matmul(b_ps[:], wb_sb[:], p_sb[:, lo : lo + T], start=True, stop=True)
                 d_ps = psum_one.tile([P, T], F32, name="d_ps")
-                nc.tensor.matmul(d_ps[:], wd_sb[:], p_sb[:], start=True, stop=True)
+                nc.tensor.matmul(d_ps[:], wd_sb[:], p_sb[:, lo : lo + T], start=True, stop=True)
                 ma_yt = work.tile([P, T], F32, name="ma_yt")
                 nc.vector.scalar_tensor_tensor(
                     ma_yt[:], a_ps[:], ua_share[:], yt_sb[:, lo : lo + T], ALU.add, ALU.mult
                 )
-                mb_y0 = work.tile([P, T], F32, name="mb_y0")
                 nc.vector.scalar_tensor_tensor(
-                    mb_y0[:], b_ps[:], ub_share[:], y0_sb[:, lo : lo + T], ALU.add, ALU.mult
+                    mb_y0[:, lo : lo + T], b_ps[:], ub_share[:], y0_sb[:, lo : lo + T], ALU.add, ALU.mult
                 )
-                md_more = work.tile([P, T], F32, name="md_more")
                 nc.vector.scalar_tensor_tensor(
-                    md_more[:], d_ps[:], ud_share[:], ma_yt[:], ALU.add, ALU.add
+                    md_more[:, lo : lo + T], d_ps[:], ud_share[:], ma_yt[:], ALU.add, ALU.add
                 )
-                mix = work.tile([P, T], F32, name="mix")
-                nc.gpsimd.tensor_tensor(mix[:], md_more[:], mb_y0[:], ALU.add)
+            mix = work.tile([P, G], F32, name="mix")
+            nc.vector.tensor_tensor(mix[:], md_more[:], mb_y0[:], ALU.add)
 
-                picked = emb_sb[:].indirect(offsets[:, j0 // 16 : (j0 + T) // 16])
-                q = work.tile([P, T], F32, name="q")
-                nc.vector.tensor_tensor(q[:], picked, mix[:], ALU.mult)
+            picked = emb_sb[:].indirect(offsets[:, j0 // 16 : (j0 + G) // 16])
+            q = work.tile([P, G], F32, name="q")
+            nc.vector.tensor_tensor(q[:], picked, mix[:], ALU.mult)
 
+            for lo in range(0, G, T):
                 mod_ps = psum_one.tile([P, T], F32, name="mod_ps")
                 for k in range(KC):
                     nc.tensor.matmul(
@@ -173,25 +168,28 @@ def tile_conditionalvelocitymodel_b_kernel(
                         stop=(k == KC - 1),
                     )
                 nc.vector.scalar_tensor_tensor(
-                    v[:, lo : lo + T], mod_ps[:], bc_plus_1[:], q[:], ALU.add, ALU.mult
+                    v[:, lo : lo + T], mod_ps[:], bc_plus_1[:], q[:, lo : lo + T], ALU.add, ALU.mult
                 )
-                nc.gpsimd.tensor_scalar(
-                    soft[:, lo : lo + T], v[:, lo : lo + T], CLAMP, -CLAMP, ALU.min, ALU.max
-                )
-                nc.scalar.activation(soft[:, lo : lo + T], soft[:, lo : lo + T], ACT.Exp)
-            nc.scalar.activation(soft[:], soft[:], ACT.Ln, bias=one_col[:])
-            for lo in range(0, CHUNK, T):
-                nc.vector.tensor_tensor(
-                    soft[:, lo : lo + T], v[:, lo : lo + T], soft[:, lo : lo + T], ALU.max
-                )
-                nc.sync.dma_start(out[:, first + lo : first + lo + T], soft[:, lo : lo + T])
+            nc.scalar.activation(soft, v, ACT.Abs)
+            nc.scalar.activation(soft, soft, ACT.Exp, scale=-1.0)
 
         routed = router(0)
         offsets = held.tile([P, N // 16], U16, name="offsets")
         nc.sync.dma_start(offsets[:], offs)
         emb_sb = held.tile([P, STEPS], F32, name="emb_sb")
         nc.sync.dma_start(emb_sb[:], emb)
-        for c in range(N // CHUNK):
-            ahead = router(c + 1) if c + 1 < N // CHUNK else None
-            experts(c, *routed)
-            routed = ahead
+        for first in range(0, GROUPS, BATCH):
+            v_all = batches.tile([P, BATCH, G], F32, name="v_all")
+            soft_all = batches.tile([P, BATCH, G], F32, name="soft_all")
+            for i in range(BATCH):
+                g = first + i
+                ahead = router(g + 1) if g + 1 < GROUPS else None
+                experts(g, *routed, v_all[:, i, :], soft_all[:, i, :])
+                routed = ahead
+            nc.scalar.activation(soft_all[:], soft_all[:], ACT.Ln, bias=one_col[:])
+            for i in range(BATCH):
+                g = first + i
+                nc.vector.scalar_tensor_tensor(
+                    soft_all[:, i, :], v_all[:, i, :], 0.0, soft_all[:, i, :], ALU.max, ALU.add
+                )
+                nc.sync.dma_start(out[:, g * G : (g + 1) * G], soft_all[:, i, :])

@@ -33,7 +33,7 @@ def tile_conditionalvelocitymodel_b_kernel(
     cov_blocks = cov.rearrange("(k p) n -> p k n", p=P)
     with (
         tc.tile_pool(name="held", bufs=1) as held,
-        tc.tile_pool(name="handed", bufs=3) as handed,
+        tc.tile_pool(name="handed", bufs=4) as handed,
         tc.tile_pool(name="work", bufs=3) as work,
         tc.tile_pool(name="batches", bufs=2) as batches,
         tc.psum_pool(name="psum_hid", bufs=2) as psum_hid,
@@ -116,60 +116,46 @@ def tile_conditionalvelocitymodel_b_kernel(
                 )
             inv_sum = work.tile([P, SPREAD], F32, name="inv_sum")
             nc.vector.reciprocal(inv_sum[:], sums_ps[:])
-            parked = out[0:1, j0 : j0 + G]
+            parked = out[P - 1 : P, j0 : j0 + G]
             nc.sync.dma_start(parked.rearrange("o (m b) -> (o m) b", b=SPREAD), inv_sum[:])
             inv_rows = handed.tile([P, G], F32, name="inv_rows")
             nc.sync.dma_start(inv_rows[:], parked.broadcast_to([P, G]))
             return cov_sb, exp_z_07, inv_rows
 
-        def experts(g, cov_sb, exp_z_07, inv_rows, v, soft):
-            j0 = g * G
-            yt_sb = work.tile([P, G], F32, name="yt_sb")
-            nc.sync.dma_start(yt_sb[:], y_t[:, j0 : j0 + G].broadcast_to([P, G]))
-            y0_sb = work.tile([P, G], F32, name="y0_sb")
-            nc.sync.dma_start(y0_sb[:], y_0_hat[:, j0 : j0 + G].broadcast_to([P, G]))
+        def experts(t, cov_sb, exp_z_07, inv_rows, v, soft):
+            j0 = t * T
+            yt_sb = work.tile([P, T], F32, name="yt_sb")
+            nc.sync.dma_start(yt_sb[:], y_t[:, j0 : j0 + T].broadcast_to([P, T]))
+            y0_sb = work.tile([P, T], F32, name="y0_sb")
+            nc.sync.dma_start(y0_sb[:], y_0_hat[:, j0 : j0 + T].broadcast_to([P, T]))
 
-            p_sb = work.tile([P, G], BF16, name="p_sb")
-            nc.vector.tensor_tensor(p_sb[:], exp_z_07[:], inv_rows[:], ALU.mult)
-            mb_y0 = work.tile([P, G], F32, name="mb_y0")
-            md_more = work.tile([P, G], F32, name="md_more")
-            for lo in range(0, G, T):
-                a_ps = psum_one.tile([P, T], F32, name="a_ps")
-                nc.tensor.matmul(a_ps[:], wa_sb[:], p_sb[:, lo : lo + T], start=True, stop=True)
-                b_ps = psum_one.tile([P, T], F32, name="b_ps")
-                nc.tensor.matmul(b_ps[:], wb_sb[:], p_sb[:, lo : lo + T], start=True, stop=True)
-                d_ps = psum_one.tile([P, T], F32, name="d_ps")
-                nc.tensor.matmul(d_ps[:], wd_sb[:], p_sb[:, lo : lo + T], start=True, stop=True)
-                ma_yt = work.tile([P, T], F32, name="ma_yt")
-                nc.vector.scalar_tensor_tensor(
-                    ma_yt[:], a_ps[:], ua_share[:], yt_sb[:, lo : lo + T], ALU.add, ALU.mult
-                )
-                nc.vector.scalar_tensor_tensor(
-                    mb_y0[:, lo : lo + T], b_ps[:], ub_share[:], y0_sb[:, lo : lo + T], ALU.add, ALU.mult
-                )
-                nc.vector.scalar_tensor_tensor(
-                    md_more[:, lo : lo + T], d_ps[:], ud_share[:], ma_yt[:], ALU.add, ALU.add
-                )
-            mix = work.tile([P, G], F32, name="mix")
+            p_sb = work.tile([P, T], BF16, name="p_sb")
+            nc.vector.tensor_tensor(p_sb[:], exp_z_07, inv_rows, ALU.mult)
+            a_ps = psum_one.tile([P, T], F32, name="a_ps")
+            nc.tensor.matmul(a_ps[:], wa_sb[:], p_sb[:], start=True, stop=True)
+            b_ps = psum_one.tile([P, T], F32, name="b_ps")
+            nc.tensor.matmul(b_ps[:], wb_sb[:], p_sb[:], start=True, stop=True)
+            d_ps = psum_one.tile([P, T], F32, name="d_ps")
+            nc.tensor.matmul(d_ps[:], wd_sb[:], p_sb[:], start=True, stop=True)
+            ma_yt = work.tile([P, T], F32, name="ma_yt")
+            nc.vector.scalar_tensor_tensor(ma_yt[:], a_ps[:], ua_share[:], yt_sb[:], ALU.add, ALU.mult)
+            mb_y0 = work.tile([P, T], F32, name="mb_y0")
+            nc.vector.scalar_tensor_tensor(mb_y0[:], b_ps[:], ub_share[:], y0_sb[:], ALU.add, ALU.mult)
+            md_more = work.tile([P, T], F32, name="md_more")
+            nc.vector.scalar_tensor_tensor(md_more[:], d_ps[:], ud_share[:], ma_yt[:], ALU.add, ALU.add)
+            mix = work.tile([P, T], F32, name="mix")
             nc.vector.tensor_tensor(mix[:], md_more[:], mb_y0[:], ALU.add)
 
-            picked = emb_sb[:].indirect(offsets[:, j0 // 16 : (j0 + G) // 16])
-            q = work.tile([P, G], F32, name="q")
+            picked = emb_sb[:].indirect(offsets[:, j0 // 16 : (j0 + T) // 16])
+            q = work.tile([P, T], F32, name="q")
             nc.vector.tensor_tensor(q[:], picked, mix[:], ALU.mult)
 
-            for lo in range(0, G, T):
-                mod_ps = psum_one.tile([P, T], F32, name="mod_ps")
-                for k in range(KC):
-                    nc.tensor.matmul(
-                        mod_ps[:],
-                        wc_sb[:, k, :],
-                        cov_sb[:, k, lo : lo + T],
-                        start=(k == 0),
-                        stop=(k == KC - 1),
-                    )
-                nc.vector.scalar_tensor_tensor(
-                    v[:, lo : lo + T], mod_ps[:], bc_plus_1[:], q[:, lo : lo + T], ALU.add, ALU.mult
+            mod_ps = psum_one.tile([P, T], F32, name="mod_ps")
+            for k in range(KC):
+                nc.tensor.matmul(
+                    mod_ps[:], wc_sb[:, k, :], cov_sb[:, k, :], start=(k == 0), stop=(k == KC - 1)
                 )
+            nc.vector.scalar_tensor_tensor(v, mod_ps[:], bc_plus_1[:], q[:], ALU.add, ALU.mult)
             nc.scalar.activation(soft, v, ACT.Abs)
             nc.scalar.activation(soft, soft, ACT.Exp, scale=-1.0)
 
@@ -179,17 +165,26 @@ def tile_conditionalvelocitymodel_b_kernel(
         emb_sb = held.tile([P, STEPS], F32, name="emb_sb")
         nc.sync.dma_start(emb_sb[:], emb)
         for first in range(0, GROUPS, BATCH):
-            v_all = batches.tile([P, BATCH, G], F32, name="v_all")
-            soft_all = batches.tile([P, BATCH, G], F32, name="soft_all")
-            for i in range(BATCH):
-                g = first + i
-                ahead = router(g + 1) if g + 1 < GROUPS else None
-                experts(g, *routed, v_all[:, i, :], soft_all[:, i, :])
-                routed = ahead
+            v_all = batches.tile([P, BATCH * G], F32, name="v_all")
+            soft_all = batches.tile([P, BATCH * G], F32, name="soft_all")
+            for g in range(first, first + BATCH):
+                cov_sb, exp_z_07, inv_rows = routed
+                if g + 1 < GROUPS:
+                    routed = router(g + 1)
+                for lo in range(0, G, T):
+                    at = (g - first) * G + lo
+                    experts(
+                        (g * G + lo) // T,
+                        cov_sb[:, :, lo : lo + T],
+                        exp_z_07[:, lo : lo + T],
+                        inv_rows[:, lo : lo + T],
+                        v_all[:, at : at + T],
+                        soft_all[:, at : at + T],
+                    )
             nc.scalar.activation(soft_all[:], soft_all[:], ACT.Ln, bias=one_col[:])
-            for i in range(BATCH):
-                g = first + i
+            for at in range(0, BATCH * G, T):
                 nc.vector.scalar_tensor_tensor(
-                    soft_all[:, i, :], v_all[:, i, :], 0.0, soft_all[:, i, :], ALU.max, ALU.add
+                    soft_all[:, at : at + T], v_all[:, at : at + T], 0.0, soft_all[:, at : at + T], ALU.max, ALU.add
                 )
-                nc.sync.dma_start(out[:, g * G : (g + 1) * G], soft_all[:, i, :])
+                j0 = first * G + at
+                nc.sync.dma_start(out[:, j0 : j0 + T], soft_all[:, at : at + T])

@@ -20,6 +20,7 @@ G = 1024
 GROUPS = N // G
 SPREAD = G // P
 BATCH = 2
+LAG = 2
 SPECIAL = 0.7
 UNIVERSAL = 0.3
 
@@ -33,7 +34,7 @@ def tile_conditionalvelocitymodel_b_kernel(
     cov_blocks = cov.rearrange("(k p) n -> p k n", p=P)
     with (
         tc.tile_pool(name="held", bufs=1) as held,
-        tc.tile_pool(name="handed", bufs=4) as handed,
+        tc.tile_pool(name="handed", bufs=LAG + 3) as handed,
         tc.tile_pool(name="work", bufs=3) as work,
         tc.tile_pool(name="batches", bufs=2) as batches,
         tc.psum_pool(name="psum_hid", bufs=2) as psum_hid,
@@ -41,7 +42,6 @@ def tile_conditionalvelocitymodel_b_kernel(
     ):
         wr1_sb = held.tile([P, KC, HID], BF16, name="wr1_sb")
         nc.sync.dma_start(wr1_sb[:], wr1.rearrange("(k p) m -> p k m", p=P))
-
         br1_sb = [held.tile([P, 1], F32, name=f"br1_sb{h}") for h in range(KH)]
         for h in range(KH):
             nc.scalar.dma_start(br1_sb[h][:], br1[h * P : (h + 1) * P, :])
@@ -49,35 +49,8 @@ def tile_conditionalvelocitymodel_b_kernel(
         nc.scalar.dma_start(wr2_sb[:], wr2.rearrange("(k p) m -> p k m", p=P))
         br2_sb = held.tile([P, 1], F32, name="br2_sb")
         nc.scalar.dma_start(br2_sb[:], br2)
-        wa_sb = held.tile([P, P], BF16, name="wa_sb")
-        nc.scalar.dma_start(wa_sb[:], wa)
-        wb_sb = held.tile([P, P], BF16, name="wb_sb")
-        nc.scalar.dma_start(wb_sb[:], wb)
-        wd_sb = held.tile([P, P], BF16, name="wd_sb")
-        nc.scalar.dma_start(wd_sb[:], wd)
-        wc_sb = held.tile([P, KC, P], BF16, name="wc_sb")
-        nc.scalar.dma_start(wc_sb[:], wc.rearrange("(k p) m -> p k m", p=P))
-        ua_sb = held.tile([P, 1], F32, name="ua_sb")
-        nc.scalar.dma_start(ua_sb[:], ua)
-        ub_sb = held.tile([P, 1], F32, name="ub_sb")
-        nc.scalar.dma_start(ub_sb[:], ub)
-        ud_sb = held.tile([P, 1], F32, name="ud_sb")
-        nc.scalar.dma_start(ud_sb[:], ud)
-        bc_sb = held.tile([P, 1], F32, name="bc_sb")
-        nc.scalar.dma_start(bc_sb[:], bc)
-
-        ua_share = held.tile([P, 1], F32, name="ua_share")
-        nc.vector.tensor_scalar_mul(ua_share[:], ua_sb[:], UNIVERSAL)
-        ub_share = held.tile([P, 1], F32, name="ub_share")
-        nc.vector.tensor_scalar_mul(ub_share[:], ub_sb[:], UNIVERSAL)
-        ud_share = held.tile([P, 1], F32, name="ud_share")
-        nc.vector.tensor_scalar_mul(ud_share[:], ud_sb[:], UNIVERSAL)
-        bc_plus_1 = held.tile([P, 1], F32, name="bc_plus_1")
-        nc.vector.tensor_scalar_add(bc_plus_1[:], bc_sb[:], 1.0)
         br2_scaled = held.tile([P, 1], F32, name="br2_scaled")
         nc.vector.tensor_scalar_add(br2_scaled[:], br2_sb[:], math.log(SPECIAL))
-        one_col = held.tile([P, 1], F32, name="one_col")
-        nc.vector.memset(one_col[:], 1.0)
         ones_bf = held.tile([P, 1], BF16, name="ones_bf")
         nc.vector.memset(ones_bf[:], 1.0)
 
@@ -159,18 +132,46 @@ def tile_conditionalvelocitymodel_b_kernel(
             nc.scalar.activation(soft, v, ACT.Abs)
             nc.scalar.activation(soft, soft, ACT.Exp, scale=-1.0)
 
-        routed = router(0)
+        routed = [router(g) for g in range(LAG)]
+
         offsets = held.tile([P, N // 16], U16, name="offsets")
         nc.sync.dma_start(offsets[:], offs)
+        wa_sb = held.tile([P, P], BF16, name="wa_sb")
+        nc.sync.dma_start(wa_sb[:], wa)
+        wb_sb = held.tile([P, P], BF16, name="wb_sb")
+        nc.sync.dma_start(wb_sb[:], wb)
+        wd_sb = held.tile([P, P], BF16, name="wd_sb")
+        nc.sync.dma_start(wd_sb[:], wd)
+        ua_sb = held.tile([P, 1], F32, name="ua_sb")
+        nc.sync.dma_start(ua_sb[:], ua)
+        ub_sb = held.tile([P, 1], F32, name="ub_sb")
+        nc.sync.dma_start(ub_sb[:], ub)
+        ud_sb = held.tile([P, 1], F32, name="ud_sb")
+        nc.sync.dma_start(ud_sb[:], ud)
         emb_sb = held.tile([P, STEPS], F32, name="emb_sb")
         nc.sync.dma_start(emb_sb[:], emb)
+        wc_sb = held.tile([P, KC, P], BF16, name="wc_sb")
+        nc.sync.dma_start(wc_sb[:], wc.rearrange("(k p) m -> p k m", p=P))
+        bc_sb = held.tile([P, 1], F32, name="bc_sb")
+        nc.sync.dma_start(bc_sb[:], bc)
+        ua_share = held.tile([P, 1], F32, name="ua_share")
+        nc.vector.tensor_scalar_mul(ua_share[:], ua_sb[:], UNIVERSAL)
+        ub_share = held.tile([P, 1], F32, name="ub_share")
+        nc.vector.tensor_scalar_mul(ub_share[:], ub_sb[:], UNIVERSAL)
+        ud_share = held.tile([P, 1], F32, name="ud_share")
+        nc.vector.tensor_scalar_mul(ud_share[:], ud_sb[:], UNIVERSAL)
+        bc_plus_1 = held.tile([P, 1], F32, name="bc_plus_1")
+        nc.vector.tensor_scalar_add(bc_plus_1[:], bc_sb[:], 1.0)
+        one_col = held.tile([P, 1], F32, name="one_col")
+        nc.vector.memset(one_col[:], 1.0)
+
         for first in range(0, GROUPS, BATCH):
             v_all = batches.tile([P, BATCH * G], F32, name="v_all")
             soft_all = batches.tile([P, BATCH * G], F32, name="soft_all")
             for g in range(first, first + BATCH):
-                cov_sb, exp_z_07, inv_rows = routed
-                if g + 1 < GROUPS:
-                    routed = router(g + 1)
+                if g + LAG < GROUPS:
+                    routed.append(router(g + LAG))
+                cov_sb, exp_z_07, inv_rows = routed[g]
                 for lo in range(0, G, T):
                     at = (g - first) * G + lo
                     experts(

@@ -103,7 +103,7 @@ def tile_conditionalvelocitymodel_b_kernel(
             nc.sync.dma_start(y0_sb[:], y_0_hat[:, j0 : j0 + T].broadcast_to([P, T]))
 
             p_sb = work.tile([P, T], BF16, name="p_sb")
-            nc.vector.tensor_tensor(p_sb[:], exp_z_07, inv_rows, ALU.mult)
+            nc.gpsimd.tensor_tensor(p_sb[:], exp_z_07, inv_rows, ALU.mult)
             a_ps = psum_one.tile([P, T], F32, name="a_ps")
             nc.tensor.matmul(a_ps[:], wa_sb[:], p_sb[:], start=True, stop=True)
             b_ps = psum_one.tile([P, T], F32, name="b_ps")

@@ -16,11 +16,11 @@ HID = 256
 KC = COV // P
 KH = HID // P
 T = 512
-G = 1024
-GROUPS = N // G
-SPREAD = G // P
-BATCH = 2
-LAG = 2
+TILES = N // T
+SPREAD = 8
+HOLDERS = T // SPREAD
+BATCH = 4
+LAG = 4
 SPECIAL = 0.7
 UNIVERSAL = 0.3
 
@@ -54,45 +54,44 @@ def tile_conditionalvelocitymodel_b_kernel(
         ones_bf = held.tile([P, 1], BF16, name="ones_bf")
         nc.vector.memset(ones_bf[:], 1.0)
 
-        def router(g):
-            j0 = g * G
-            cov_sb = handed.tile([P, KC, G], BF16, name="cov_sb")
-            exp_z = work.tile([P, G], BF16, name="exp_z")
-            exp_z_07 = handed.tile([P, G], F32, name="exp_z_07")
-            for lo in range(0, G, T):
-                nc.sync.dma_start(cov_sb[:, :, lo : lo + T], cov_blocks[:, :, j0 + lo : j0 + lo + T])
-                hid_sb = work.tile([P, KH, T], BF16, name="hid_sb")
-                for h in range(KH):
-                    hid_ps = psum_hid.tile([P, T], F32, name="hid_ps")
-                    for k in range(KC):
-                        nc.tensor.matmul(
-                            hid_ps[:],
-                            wr1_sb[:, k, h * P : (h + 1) * P],
-                            cov_sb[:, k, lo : lo + T],
-                            start=(k == 0),
-                            stop=(k == KC - 1),
-                        )
-                    nc.scalar.activation(hid_sb[:, h, :], hid_ps[:], ACT.Relu, bias=br1_sb[h][:])
-                z_ps = psum_one.tile([P, T], F32, name="z_ps")
-                for h in range(KH):
+        def router(t):
+            j0 = t * T
+            cov_sb = handed.tile([P, KC, T], BF16, name="cov_sb")
+            nc.sync.dma_start(cov_sb[:], cov_blocks[:, :, j0 : j0 + T])
+            hid_sb = work.tile([P, KH, T], BF16, name="hid_sb")
+            for h in range(KH):
+                hid_ps = psum_hid.tile([P, T], F32, name="hid_ps")
+                for k in range(KC):
                     nc.tensor.matmul(
-                        z_ps[:], wr2_sb[:, h, :], hid_sb[:, h, :], start=(h == 0), stop=(h == KH - 1)
+                        hid_ps[:],
+                        wr1_sb[:, k, h * P : (h + 1) * P],
+                        cov_sb[:, k, :],
+                        start=(k == 0),
+                        stop=(k == KC - 1),
                     )
-                nc.scalar.activation(exp_z[:, lo : lo + T], z_ps[:], ACT.Exp, bias=br2_sb[:])
-                nc.scalar.activation(exp_z_07[:, lo : lo + T], z_ps[:], ACT.Exp, bias=br2_scaled[:])
+                nc.scalar.activation(hid_sb[:, h, :], hid_ps[:], ACT.Relu, bias=br1_sb[h][:])
+            z_ps = psum_one.tile([P, T], F32, name="z_ps")
+            for h in range(KH):
+                nc.tensor.matmul(
+                    z_ps[:], wr2_sb[:, h, :], hid_sb[:, h, :], start=(h == 0), stop=(h == KH - 1)
+                )
+            exp_z = work.tile([P, T], BF16, name="exp_z")
+            nc.scalar.activation(exp_z[:], z_ps[:], ACT.Exp, bias=br2_sb[:])
+            exp_z_07 = handed.tile([P, T], F32, name="exp_z_07")
+            nc.scalar.activation(exp_z_07[:], z_ps[:], ACT.Exp, bias=br2_scaled[:])
 
-            sums_ps = psum_one.tile([P, SPREAD], F32, name="sums_ps")
+            sums_ps = psum_one.tile([HOLDERS, SPREAD], F32, name="sums_ps")
             every_spread = exp_z[:].rearrange("e (m b) -> e b m", b=SPREAD)
             for b in range(SPREAD):
                 nc.tensor.matmul(
                     sums_ps[:, b : b + 1], every_spread[:, b, :], ones_bf[:], start=True, stop=True
                 )
-            inv_sum = work.tile([P, SPREAD], F32, name="inv_sum")
+            inv_sum = work.tile([HOLDERS, SPREAD], F32, name="inv_sum")
             nc.vector.reciprocal(inv_sum[:], sums_ps[:])
-            parked = out[P - 1 : P, j0 : j0 + G]
+            parked = out[P - 1 : P, j0 : j0 + T]
             nc.sync.dma_start(parked.rearrange("o (m b) -> (o m) b", b=SPREAD), inv_sum[:])
-            inv_rows = handed.tile([P, G], F32, name="inv_rows")
-            nc.sync.dma_start(inv_rows[:], parked.broadcast_to([P, G]))
+            inv_rows = handed.tile([P, T], F32, name="inv_rows")
+            nc.sync.dma_start(inv_rows[:], parked.broadcast_to([P, T]))
             return cov_sb, exp_z_07, inv_rows
 
         def experts(t, cov_sb, exp_z_07, inv_rows, v, soft):
@@ -103,7 +102,7 @@ def tile_conditionalvelocitymodel_b_kernel(
             nc.sync.dma_start(y0_sb[:], y_0_hat[:, j0 : j0 + T].broadcast_to([P, T]))
 
             p_sb = work.tile([P, T], BF16, name="p_sb")
-            nc.gpsimd.tensor_tensor(p_sb[:], exp_z_07, inv_rows, ALU.mult)
+            nc.gpsimd.tensor_tensor(p_sb[:], exp_z_07[:], inv_rows[:], ALU.mult)
             a_ps = psum_one.tile([P, T], F32, name="a_ps")
             nc.tensor.matmul(a_ps[:], wa_sb[:], p_sb[:], start=True, stop=True)
             b_ps = psum_one.tile([P, T], F32, name="b_ps")
@@ -132,7 +131,7 @@ def tile_conditionalvelocitymodel_b_kernel(
             nc.scalar.activation(soft, v, ACT.Abs)
             nc.scalar.activation(soft, soft, ACT.Exp, scale=-1.0)
 
-        routed = [router(g) for g in range(LAG)]
+        routed = [router(t) for t in range(LAG)]
 
         offsets = held.tile([P, N // 16], U16, name="offsets")
         nc.sync.dma_start(offsets[:], offs)
@@ -165,27 +164,18 @@ def tile_conditionalvelocitymodel_b_kernel(
         one_col = held.tile([P, 1], F32, name="one_col")
         nc.vector.memset(one_col[:], 1.0)
 
-        for first in range(0, GROUPS, BATCH):
-            v_all = batches.tile([P, BATCH * G], F32, name="v_all")
-            soft_all = batches.tile([P, BATCH * G], F32, name="soft_all")
-            for g in range(first, first + BATCH):
-                if g + LAG < GROUPS:
-                    routed.append(router(g + LAG))
-                cov_sb, exp_z_07, inv_rows = routed[g]
-                for lo in range(0, G, T):
-                    at = (g - first) * G + lo
-                    experts(
-                        (g * G + lo) // T,
-                        cov_sb[:, :, lo : lo + T],
-                        exp_z_07[:, lo : lo + T],
-                        inv_rows[:, lo : lo + T],
-                        v_all[:, at : at + T],
-                        soft_all[:, at : at + T],
-                    )
+        for first in range(0, TILES, BATCH):
+            v_all = batches.tile([P, BATCH, T], F32, name="v_all")
+            soft_all = batches.tile([P, BATCH, T], F32, name="soft_all")
+            for i in range(BATCH):
+                t = first + i
+                if t + LAG < TILES:
+                    routed.append(router(t + LAG))
+                experts(t, *routed[t], v_all[:, i, :], soft_all[:, i, :])
             nc.scalar.activation(soft_all[:], soft_all[:], ACT.Ln, bias=one_col[:])
-            for at in range(0, BATCH * G, T):
+            for i in range(BATCH):
+                t = first + i
                 nc.vector.scalar_tensor_tensor(
-                    soft_all[:, at : at + T], v_all[:, at : at + T], 0.0, soft_all[:, at : at + T], ALU.max, ALU.add
+                    soft_all[:, i, :], v_all[:, i, :], 0.0, soft_all[:, i, :], ALU.max, ALU.add
                 )
-                j0 = first * G + at
-                nc.sync.dma_start(out[:, j0 : j0 + T], soft_all[:, at : at + T])
+                nc.sync.dma_start(out[:, t * T : (t + 1) * T], soft_all[:, i, :])

@@ -16,11 +16,11 @@ HID = 256
 KC = COV // P
 KH = HID // P
 T = 512
-TILES = N // T
-SPREAD = 8
-HOLDERS = T // SPREAD
-BATCH = 4
-LAG = 4
+G = 1024
+GROUPS = N // G
+SPREAD = G // P
+BATCH = 2
+LAG = 2
 SPECIAL = 0.7
 UNIVERSAL = 0.3
 
@@ -35,6 +35,7 @@ def tile_conditionalvelocitymodel_b_kernel(
     with (
         tc.tile_pool(name="held", bufs=1) as held,
         tc.tile_pool(name="handed", bufs=LAG + 3) as handed,
+        tc.tile_pool(name="rows", bufs=3) as rows,
         tc.tile_pool(name="work", bufs=3) as work,
         tc.tile_pool(name="batches", bufs=2) as batches,
         tc.psum_pool(name="psum_hid", bufs=2) as psum_hid,
@@ -54,55 +55,51 @@ def tile_conditionalvelocitymodel_b_kernel(
         ones_bf = held.tile([P, 1], BF16, name="ones_bf")
         nc.vector.memset(ones_bf[:], 1.0)
 
-        def router(t):
-            j0 = t * T
-            cov_sb = handed.tile([P, KC, T], BF16, name="cov_sb")
-            nc.sync.dma_start(cov_sb[:], cov_blocks[:, :, j0 : j0 + T])
-            hid_sb = work.tile([P, KH, T], BF16, name="hid_sb")
-            for h in range(KH):
-                hid_ps = psum_hid.tile([P, T], F32, name="hid_ps")
-                for k in range(KC):
+        def router(g):
+            j0 = g * G
+            cov_sb = handed.tile([P, KC, G], BF16, name="cov_sb")
+            exp_z = work.tile([P, G], BF16, name="exp_z")
+            exp_z_07 = handed.tile([P, G], F32, name="exp_z_07")
+            for lo in range(0, G, T):
+                nc.sync.dma_start(cov_sb[:, :, lo : lo + T], cov_blocks[:, :, j0 + lo : j0 + lo + T])
+                hid_sb = work.tile([P, KH, T], BF16, name="hid_sb")
+                for h in range(KH):
+                    hid_ps = psum_hid.tile([P, T], F32, name="hid_ps")
+                    for k in range(KC):
+                        nc.tensor.matmul(
+                            hid_ps[:],
+                            wr1_sb[:, k, h * P : (h + 1) * P],
+                            cov_sb[:, k, lo : lo + T],
+                            start=(k == 0),
+                            stop=(k == KC - 1),
+                        )
+                    nc.scalar.activation(hid_sb[:, h, :], hid_ps[:], ACT.Relu, bias=br1_sb[h][:])
+                z_ps = psum_one.tile([P, T], F32, name="z_ps")
+                for h in range(KH):
                     nc.tensor.matmul(
-                        hid_ps[:],
-                        wr1_sb[:, k, h * P : (h + 1) * P],
-                        cov_sb[:, k, :],
-                        start=(k == 0),
-                        stop=(k == KC - 1),
+                        z_ps[:], wr2_sb[:, h, :], hid_sb[:, h, :], start=(h == 0), stop=(h == KH - 1)
                     )
-                nc.scalar.activation(hid_sb[:, h, :], hid_ps[:], ACT.Relu, bias=br1_sb[h][:])
-            z_ps = psum_one.tile([P, T], F32, name="z_ps")
-            for h in range(KH):
-                nc.tensor.matmul(
-                    z_ps[:], wr2_sb[:, h, :], hid_sb[:, h, :], start=(h == 0), stop=(h == KH - 1)
-                )
-            exp_z = work.tile([P, T], BF16, name="exp_z")
-            nc.scalar.activation(exp_z[:], z_ps[:], ACT.Exp, bias=br2_sb[:])
-            exp_z_07 = handed.tile([P, T], F32, name="exp_z_07")
-            nc.scalar.activation(exp_z_07[:], z_ps[:], ACT.Exp, bias=br2_scaled[:])
+                nc.scalar.activation(exp_z[:, lo : lo + T], z_ps[:], ACT.Exp, bias=br2_sb[:])
+                nc.scalar.activation(exp_z_07[:, lo : lo + T], z_ps[:], ACT.Exp, bias=br2_scaled[:])
 
-            sums_ps = psum_one.tile([HOLDERS, SPREAD], F32, name="sums_ps")
+            sums_ps = psum_one.tile([P, SPREAD], F32, name="sums_ps")
             every_spread = exp_z[:].rearrange("e (m b) -> e b m", b=SPREAD)
             for b in range(SPREAD):
                 nc.tensor.matmul(
                     sums_ps[:, b : b + 1], every_spread[:, b, :], ones_bf[:], start=True, stop=True
                 )
-            inv_sum = work.tile([HOLDERS, SPREAD], F32, name="inv_sum")
+            inv_sum = work.tile([P, SPREAD], F32, name="inv_sum")
             nc.vector.reciprocal(inv_sum[:], sums_ps[:])
-            parked = out[P - 1 : P, j0 : j0 + T]
+            parked = out[P - 1 : P, j0 : j0 + G]
             nc.sync.dma_start(parked.rearrange("o (m b) -> (o m) b", b=SPREAD), inv_sum[:])
-            inv_rows = handed.tile([P, T], F32, name="inv_rows")
-            nc.sync.dma_start(inv_rows[:], parked.broadcast_to([P, T]))
+            inv_rows = handed.tile([P, G], F32, name="inv_rows")
+            nc.sync.dma_start(inv_rows[:], parked.broadcast_to([P, G]))
             return cov_sb, exp_z_07, inv_rows
 
-        def experts(t, cov_sb, exp_z_07, inv_rows, v, soft):
+        def experts(t, cov_sb, exp_z_07, inv_rows, yt_sb, y0_sb, v, soft):
             j0 = t * T
-            yt_sb = work.tile([P, T], F32, name="yt_sb")
-            nc.sync.dma_start(yt_sb[:], y_t[:, j0 : j0 + T].broadcast_to([P, T]))
-            y0_sb = work.tile([P, T], F32, name="y0_sb")
-            nc.sync.dma_start(y0_sb[:], y_0_hat[:, j0 : j0 + T].broadcast_to([P, T]))
-
             p_sb = work.tile([P, T], BF16, name="p_sb")
-            nc.gpsimd.tensor_tensor(p_sb[:], exp_z_07[:], inv_rows[:], ALU.mult)
+            nc.gpsimd.tensor_tensor(p_sb[:], exp_z_07, inv_rows, ALU.mult)
             a_ps = psum_one.tile([P, T], F32, name="a_ps")
             nc.tensor.matmul(a_ps[:], wa_sb[:], p_sb[:], start=True, stop=True)
             b_ps = psum_one.tile([P, T], F32, name="b_ps")
@@ -110,9 +107,9 @@ def tile_conditionalvelocitymodel_b_kernel(
             d_ps = psum_one.tile([P, T], F32, name="d_ps")
             nc.tensor.matmul(d_ps[:], wd_sb[:], p_sb[:], start=True, stop=True)
             ma_yt = work.tile([P, T], F32, name="ma_yt")
-            nc.vector.scalar_tensor_tensor(ma_yt[:], a_ps[:], ua_share[:], yt_sb[:], ALU.add, ALU.mult)
+            nc.vector.scalar_tensor_tensor(ma_yt[:], a_ps[:], ua_share[:], yt_sb, ALU.add, ALU.mult)
             mb_y0 = work.tile([P, T], F32, name="mb_y0")
-            nc.vector.scalar_tensor_tensor(mb_y0[:], b_ps[:], ub_share[:], y0_sb[:], ALU.add, ALU.mult)
+            nc.vector.scalar_tensor_tensor(mb_y0[:], b_ps[:], ub_share[:], y0_sb, ALU.add, ALU.mult)
             md_more = work.tile([P, T], F32, name="md_more")
             nc.vector.scalar_tensor_tensor(md_more[:], d_ps[:], ud_share[:], ma_yt[:], ALU.add, ALU.add)
             mix = work.tile([P, T], F32, name="mix")
@@ -131,7 +128,7 @@ def tile_conditionalvelocitymodel_b_kernel(
             nc.scalar.activation(soft, v, ACT.Abs)
             nc.scalar.activation(soft, soft, ACT.Exp, scale=-1.0)
 
-        routed = [router(t) for t in range(LAG)]
+        routed = [router(g) for g in range(LAG)]
 
         offsets = held.tile([P, N // 16], U16, name="offsets")
         nc.sync.dma_start(offsets[:], offs)
@@ -164,18 +161,33 @@ def tile_conditionalvelocitymodel_b_kernel(
         one_col = held.tile([P, 1], F32, name="one_col")
         nc.vector.memset(one_col[:], 1.0)
 
-        for first in range(0, TILES, BATCH):
-            v_all = batches.tile([P, BATCH, T], F32, name="v_all")
-            soft_all = batches.tile([P, BATCH, T], F32, name="soft_all")
-            for i in range(BATCH):
-                t = first + i
-                if t + LAG < TILES:
-                    routed.append(router(t + LAG))
-                experts(t, *routed[t], v_all[:, i, :], soft_all[:, i, :])
+        for first in range(0, GROUPS, BATCH):
+            v_all = batches.tile([P, BATCH * G], F32, name="v_all")
+            soft_all = batches.tile([P, BATCH * G], F32, name="soft_all")
+            for g in range(first, first + BATCH):
+                if g + LAG < GROUPS:
+                    routed.append(router(g + LAG))
+                cov_sb, exp_z_07, inv_rows = routed[g]
+                yt_sb = rows.tile([P, G], F32, name="yt_sb")
+                nc.sync.dma_start(yt_sb[:], y_t[:, g * G : (g + 1) * G].broadcast_to([P, G]))
+                y0_sb = rows.tile([P, G], F32, name="y0_sb")
+                nc.sync.dma_start(y0_sb[:], y_0_hat[:, g * G : (g + 1) * G].broadcast_to([P, G]))
+                for lo in range(0, G, T):
+                    at = (g - first) * G + lo
+                    experts(
+                        (g * G + lo) // T,
+                        cov_sb[:, :, lo : lo + T],
+                        exp_z_07[:, lo : lo + T],
+                        inv_rows[:, lo : lo + T],
+                        yt_sb[:, lo : lo + T],
+                        y0_sb[:, lo : lo + T],
+                        v_all[:, at : at + T],
+                        soft_all[:, at : at + T],
+                    )
             nc.scalar.activation(soft_all[:], soft_all[:], ACT.Ln, bias=one_col[:])
-            for i in range(BATCH):
-                t = first + i
+            for at in range(0, BATCH * G, G):
                 nc.vector.scalar_tensor_tensor(
-                    soft_all[:, i, :], v_all[:, i, :], 0.0, soft_all[:, i, :], ALU.max, ALU.add
+                    soft_all[:, at : at + G], v_all[:, at : at + G], 0.0, soft_all[:, at : at + G], ALU.max, ALU.add
                 )
-                nc.sync.dma_start(out[:, t * T : (t + 1) * T], soft_all[:, i, :])
+                j0 = first * G + at
+                nc.sync.dma_start(out[:, j0 : j0 + G], soft_all[:, at : at + G])

@@ -19,7 +19,7 @@ T = 512
 G = 1024
 GROUPS = N // G
 SPREAD = G // P
-BATCH = 2
+BATCHES = (7, 1)
 LAG = 2
 SPECIAL = 0.7
 UNIVERSAL = 0.3
@@ -37,7 +37,6 @@ def tile_conditionalvelocitymodel_b_kernel(
         tc.tile_pool(name="handed", bufs=LAG + 3) as handed,
         tc.tile_pool(name="rows", bufs=3) as rows,
         tc.tile_pool(name="work", bufs=3) as work,
-        tc.tile_pool(name="batches", bufs=2) as batches,
         tc.psum_pool(name="psum_hid", bufs=2) as psum_hid,
         tc.psum_pool(name="psum_one", bufs=1) as psum_one,
     ):
@@ -161,10 +160,10 @@ def tile_conditionalvelocitymodel_b_kernel(
         one_col = held.tile([P, 1], F32, name="one_col")
         nc.vector.memset(one_col[:], 1.0)
 
-        for first in range(0, GROUPS, BATCH):
-            v_all = batches.tile([P, BATCH * G], F32, name="v_all")
-            soft_all = batches.tile([P, BATCH * G], F32, name="soft_all")
-            for g in range(first, first + BATCH):
+        v_all = held.tile([P, N], F32, name="v_all")
+        soft_all = held.tile([P, N], F32, name="soft_all")
+        for first, groups in zip((0, BATCHES[0]), BATCHES):
+            for g in range(first, first + groups):
                 if g + LAG < GROUPS:
                     routed.append(router(g + LAG))
                 cov_sb, exp_z_07, inv_rows = routed[g]
@@ -173,7 +172,7 @@ def tile_conditionalvelocitymodel_b_kernel(
                 y0_sb = rows.tile([P, G], F32, name="y0_sb")
                 nc.sync.dma_start(y0_sb[:], y_0_hat[:, g * G : (g + 1) * G].broadcast_to([P, G]))
                 for lo in range(0, G, T):
-                    at = (g - first) * G + lo
+                    at = g * G + lo
                     experts(
                         (g * G + lo) // T,
                         cov_sb[:, :, lo : lo + T],
@@ -184,10 +183,10 @@ def tile_conditionalvelocitymodel_b_kernel(
                         v_all[:, at : at + T],
                         soft_all[:, at : at + T],
                     )
-            nc.scalar.activation(soft_all[:], soft_all[:], ACT.Ln, bias=one_col[:])
-            for at in range(0, BATCH * G, G):
+            batch = slice(first * G, (first + groups) * G)
+            nc.scalar.activation(soft_all[:, batch], soft_all[:, batch], ACT.Ln, bias=one_col[:])
+            for at in range(batch.start, batch.stop, G):
                 nc.vector.scalar_tensor_tensor(
                     soft_all[:, at : at + G], v_all[:, at : at + G], 0.0, soft_all[:, at : at + G], ALU.max, ALU.add
                 )
-                j0 = first * G + at
-                nc.sync.dma_start(out[:, j0 : j0 + G], soft_all[:, at : at + G])
+                nc.sync.dma_start(out[:, at : at + G], soft_all[:, at : at + G])

@@ -19,8 +19,8 @@ T = 512
 G = 1024
 GROUPS = N // G
 SPREAD = G // P
-BATCHES = (7, 1)
 LAG = 2
+BATCHES = (GROUPS - LAG, LAG)
 SPECIAL = 0.7
 UNIVERSAL = 0.3
 
@@ -185,8 +185,8 @@ def tile_conditionalvelocitymodel_b_kernel(
                     )
             batch = slice(first * G, (first + groups) * G)
             nc.scalar.activation(soft_all[:, batch], soft_all[:, batch], ACT.Ln, bias=one_col[:])
-            for at in range(batch.start, batch.stop, G):
-                nc.vector.scalar_tensor_tensor(
-                    soft_all[:, at : at + G], v_all[:, at : at + G], 0.0, soft_all[:, at : at + G], ALU.max, ALU.add
-                )
-                nc.sync.dma_start(out[:, at : at + G], soft_all[:, at : at + G])
+        for at in range(0, N, T):
+            nc.vector.scalar_tensor_tensor(
+                soft_all[:, at : at + T], v_all[:, at : at + T], 0.0, soft_all[:, at : at + T], ALU.max, ALU.add
+            )
+            nc.sync.dma_start(out[:, at : at + T], soft_all[:, at : at + T])

@@ -57,7 +57,7 @@ def tile_conditionalvelocitymodel_b_kernel(
         def router(g):
             j0 = g * G
             cov_sb = handed.tile([P, KC, G], BF16, name="cov_sb")
-            exp_z = work.tile([P, G], BF16, name="exp_z")
+            exp_z = work.tile([P, SPREAD, P], BF16, name="exp_z")
             exp_z_07 = handed.tile([P, G], F32, name="exp_z_07")
             for lo in range(0, G, T):
                 nc.sync.dma_start(cov_sb[:, :, lo : lo + T], cov_blocks[:, :, j0 + lo : j0 + lo + T])
@@ -78,15 +78,17 @@ def tile_conditionalvelocitymodel_b_kernel(
                     nc.tensor.matmul(
                         z_ps[:], wr2_sb[:, h, :], hid_sb[:, h, :], start=(h == 0), stop=(h == KH - 1)
                     )
-                nc.scalar.activation(exp_z[:, lo : lo + T], z_ps[:], ACT.Exp, bias=br2_sb[:])
+                nc.scalar.activation(
+                    exp_z[:, :, lo // SPREAD : (lo + T) // SPREAD],
+                    z_ps[:].rearrange("e (m b) -> e b m", b=SPREAD),
+                    ACT.Exp,
+                    bias=br2_sb[:],
+                )
                 nc.scalar.activation(exp_z_07[:, lo : lo + T], z_ps[:], ACT.Exp, bias=br2_scaled[:])
 
             sums_ps = psum_one.tile([P, SPREAD], F32, name="sums_ps")
-            every_spread = exp_z[:].rearrange("e (m b) -> e b m", b=SPREAD)
             for b in range(SPREAD):
-                nc.tensor.matmul(
-                    sums_ps[:, b : b + 1], every_spread[:, b, :], ones_bf[:], start=True, stop=True
-                )
+                nc.tensor.matmul(sums_ps[:, b : b + 1], exp_z[:, b, :], ones_bf[:], start=True, stop=True)
             inv_sum = work.tile([P, SPREAD], F32, name="inv_sum")
             nc.vector.reciprocal(inv_sum[:], sums_ps[:])
             parked = out[P - 1 : P, j0 : j0 + G]

@@ -18,6 +18,7 @@ KH = HID // P
 T = 512
 G = 1024
 GROUPS = N // G
+TILES = N // T
 SPREAD = G // P
 LAG = 2
 BATCHES = (GROUPS - LAG, LAG)
@@ -97,35 +98,74 @@ def tile_conditionalvelocitymodel_b_kernel(
             nc.sync.dma_start(inv_rows[:], parked.broadcast_to([P, G]))
             return cov_sb, exp_z_07, inv_rows
 
-        def experts(t, cov_sb, exp_z_07, inv_rows, yt_sb, y0_sb, v, soft):
-            j0 = t * T
+        rows_of = {}
+        parts = {}
+
+        def spot(t):
+            g, lo = divmod(t * T, G)
+            return g, slice(lo, lo + T)
+
+        def weigh(t):
+            g, cols = spot(t)
+            if cols.start == 0:
+                yt_sb = rows.tile([P, G], F32, name="yt_sb")
+                nc.sync.dma_start(yt_sb[:], y_t[:, g * G : (g + 1) * G].broadcast_to([P, G]))
+                y0_sb = rows.tile([P, G], F32, name="y0_sb")
+                nc.sync.dma_start(y0_sb[:], y_0_hat[:, g * G : (g + 1) * G].broadcast_to([P, G]))
+                rows_of[g] = (yt_sb, y0_sb)
+            cov_sb, exp_z_07, inv_rows = routed[g]
             p_sb = work.tile([P, T], BF16, name="p_sb")
-            nc.gpsimd.tensor_tensor(p_sb[:], exp_z_07, inv_rows, ALU.mult)
+            nc.gpsimd.tensor_tensor(p_sb[:], exp_z_07[:, cols], inv_rows[:, cols], ALU.mult)
+            parts[t] = {"p": p_sb}
+
+        def share_a(t):
+            g, cols = spot(t)
             a_ps = psum_one.tile([P, T], F32, name="a_ps")
-            nc.tensor.matmul(a_ps[:], wa_sb[:], p_sb[:], start=True, stop=True)
-            b_ps = psum_one.tile([P, T], F32, name="b_ps")
-            nc.tensor.matmul(b_ps[:], wb_sb[:], p_sb[:], start=True, stop=True)
-            d_ps = psum_one.tile([P, T], F32, name="d_ps")
-            nc.tensor.matmul(d_ps[:], wd_sb[:], p_sb[:], start=True, stop=True)
+            nc.tensor.matmul(a_ps[:], wa_sb[:], parts[t]["p"][:], start=True, stop=True)
             ma_yt = work.tile([P, T], F32, name="ma_yt")
-            nc.vector.scalar_tensor_tensor(ma_yt[:], a_ps[:], ua_share[:], yt_sb, ALU.add, ALU.mult)
+            nc.vector.scalar_tensor_tensor(ma_yt[:], a_ps[:], ua_share[:], rows_of[g][0][:, cols], ALU.add, ALU.mult)
+            parts[t]["ma_yt"] = ma_yt
+
+        def share_b(t):
+            g, cols = spot(t)
+            b_ps = psum_one.tile([P, T], F32, name="b_ps")
+            nc.tensor.matmul(b_ps[:], wb_sb[:], parts[t]["p"][:], start=True, stop=True)
             mb_y0 = work.tile([P, T], F32, name="mb_y0")
-            nc.vector.scalar_tensor_tensor(mb_y0[:], b_ps[:], ub_share[:], y0_sb, ALU.add, ALU.mult)
+            nc.vector.scalar_tensor_tensor(mb_y0[:], b_ps[:], ub_share[:], rows_of[g][1][:, cols], ALU.add, ALU.mult)
+            parts[t]["mb_y0"] = mb_y0
+
+        def share_d(t):
+            d_ps = psum_one.tile([P, T], F32, name="d_ps")
+            nc.tensor.matmul(d_ps[:], wd_sb[:], parts[t]["p"][:], start=True, stop=True)
             md_more = work.tile([P, T], F32, name="md_more")
-            nc.vector.scalar_tensor_tensor(md_more[:], d_ps[:], ud_share[:], ma_yt[:], ALU.add, ALU.add)
-            mix = work.tile([P, T], F32, name="mix")
-            nc.vector.tensor_tensor(mix[:], md_more[:], mb_y0[:], ALU.add)
+            nc.vector.scalar_tensor_tensor(md_more[:], d_ps[:], ud_share[:], parts[t]["ma_yt"][:], ALU.add, ALU.add)
+            parts[t]["md_more"] = md_more
 
-            picked = emb_sb[:].indirect(offsets[:, j0 // 16 : (j0 + T) // 16])
-            q = work.tile([P, T], F32, name="q")
-            nc.vector.tensor_tensor(q[:], picked, mix[:], ALU.mult)
-
+        def project(t):
+            g, cols = spot(t)
+            cov_sb = routed[g][0]
             mod_ps = psum_one.tile([P, T], F32, name="mod_ps")
             for k in range(KC):
                 nc.tensor.matmul(
-                    mod_ps[:], wc_sb[:, k, :], cov_sb[:, k, :], start=(k == 0), stop=(k == KC - 1)
+                    mod_ps[:], wc_sb[:, k, :], cov_sb[:, k, cols], start=(k == 0), stop=(k == KC - 1)
                 )
-            nc.vector.scalar_tensor_tensor(v, mod_ps[:], bc_plus_1[:], q[:], ALU.add, ALU.mult)
+            parts[t]["mod"] = mod_ps
+
+        def add_up(t):
+            mix = work.tile([P, T], F32, name="mix")
+            nc.vector.tensor_tensor(mix[:], parts[t]["md_more"][:], parts[t]["mb_y0"][:], ALU.add)
+            parts[t]["mix"] = mix
+
+        def look_up(t):
+            picked = emb_sb[:].indirect(offsets[:, t * T // 16 : (t + 1) * T // 16])
+            q = work.tile([P, T], F32, name="q")
+            nc.vector.tensor_tensor(q[:], picked, parts[t]["mix"][:], ALU.mult)
+            parts[t]["q"] = q
+
+        def modulate(t):
+            v = v_all[:, t * T : (t + 1) * T]
+            soft = soft_all[:, t * T : (t + 1) * T]
+            nc.vector.scalar_tensor_tensor(v, parts[t]["mod"][:], bc_plus_1[:], parts[t]["q"][:], ALU.add, ALU.mult)
             nc.scalar.activation(soft, v, ACT.Abs)
             nc.scalar.activation(soft, soft, ACT.Exp, scale=-1.0)
 
@@ -164,28 +204,29 @@ def tile_conditionalvelocitymodel_b_kernel(
 
         v_all = held.tile([P, N], F32, name="v_all")
         soft_all = held.tile([P, N], F32, name="soft_all")
-        for first, groups in zip((0, BATCHES[0]), BATCHES):
-            for g in range(first, first + groups):
-                if g + LAG < GROUPS:
-                    routed.append(router(g + LAG))
-                cov_sb, exp_z_07, inv_rows = routed[g]
-                yt_sb = rows.tile([P, G], F32, name="yt_sb")
-                nc.sync.dma_start(yt_sb[:], y_t[:, g * G : (g + 1) * G].broadcast_to([P, G]))
-                y0_sb = rows.tile([P, G], F32, name="y0_sb")
-                nc.sync.dma_start(y0_sb[:], y_0_hat[:, g * G : (g + 1) * G].broadcast_to([P, G]))
-                for lo in range(0, G, T):
-                    at = g * G + lo
-                    experts(
-                        (g * G + lo) // T,
-                        cov_sb[:, :, lo : lo + T],
-                        exp_z_07[:, lo : lo + T],
-                        inv_rows[:, lo : lo + T],
-                        yt_sb[:, lo : lo + T],
-                        y0_sb[:, lo : lo + T],
-                        v_all[:, at : at + T],
-                        soft_all[:, at : at + T],
-                    )
-            batch = slice(first * G, (first + groups) * G)
+        routed.append(router(LAG))
+        weigh(0)
+        share_a(0)
+        share_b(0)
+        share_d(0)
+        for first, tiles in zip((0, BATCHES[0] * G // T), (BATCHES[0] * G // T, BATCHES[1] * G // T)):
+            for t in range(first, first + tiles):
+                more = t + 1 < TILES
+                g_next, cols_next = spot(t + 1)
+                if cols_next.start == 0 and g_next + LAG < GROUPS:
+                    routed.append(router(g_next + LAG))
+                project(t)
+                if more:
+                    weigh(t + 1)
+                    share_a(t + 1)
+                add_up(t)
+                if more:
+                    share_b(t + 1)
+                look_up(t)
+                if more:
+                    share_d(t + 1)
+                modulate(t)
+            batch = slice(first * T, (first + tiles) * T)
             nc.scalar.activation(soft_all[:, batch], soft_all[:, batch], ACT.Ln, bias=one_col[:])
         for at in range(0, N, T):
             nc.vector.scalar_tensor_tensor(

@@ -35,9 +35,9 @@ def tile_conditionalvelocitymodel_b_kernel(
     cov_blocks = cov.rearrange("(k p) n -> p k n", p=P)
     with (
         tc.tile_pool(name="held", bufs=1) as held,
-        tc.tile_pool(name="handed", bufs=LAG + 3) as handed,
+        tc.tile_pool(name="handed", bufs=LAG + 2) as handed,
         tc.tile_pool(name="rows", bufs=3) as rows,
-        tc.tile_pool(name="work", bufs=3) as work,
+        tc.tile_pool(name="work", bufs=2) as work,
         tc.psum_pool(name="psum_hid", bufs=2) as psum_hid,
         tc.psum_pool(name="psum_one", bufs=1) as psum_one,
     ):
@@ -55,9 +55,11 @@ def tile_conditionalvelocitymodel_b_kernel(
         ones_bf = held.tile([P, 1], BF16, name="ones_bf")
         nc.vector.memset(ones_bf[:], 1.0)
 
+        cov_all = held.tile([P, KC, N], BF16, name="cov_all")
+
         def router(g):
             j0 = g * G
-            cov_sb = handed.tile([P, KC, G], BF16, name="cov_sb")
+            cov_sb = cov_all[:, :, j0 : j0 + G]
             exp_z = work.tile([P, SPREAD, P], BF16, name="exp_z")
             exp_z_07 = handed.tile([P, G], F32, name="exp_z_07")
             for lo in range(0, G, T):

@@ -37,7 +37,7 @@ def tile_conditionalvelocitymodel_b_kernel(
         tc.tile_pool(name="held", bufs=1) as held,
         tc.tile_pool(name="handed", bufs=LAG + 2) as handed,
         tc.tile_pool(name="rows", bufs=3) as rows,
-        tc.tile_pool(name="work", bufs=2) as work,
+        tc.tile_pool(name="work", bufs=3) as work,
         tc.psum_pool(name="psum_hid", bufs=2) as psum_hid,
         tc.psum_pool(name="psum_one", bufs=1) as psum_one,
     ):

import math

import concourse.mybir as mybir

F32 = mybir.dt.float32
BF16 = mybir.dt.bfloat16
U16 = mybir.dt.uint16
ALU = mybir.AluOpType
ACT = mybir.ActivationFunctionType

P = 128
STEPS = 1024
N = 8192
COV = 512
HID = 256
KC = COV // P
KH = HID // P
T = 512
G = 1024
GROUPS = N // G
TILES = N // T
SPREAD = G // P
LAG = 2
BATCHES = (GROUPS - LAG, LAG)
SPECIAL = 0.7
UNIVERSAL = 0.3

FLOPS = 2 * N * (COV * HID + HID * P + COV * P + 3 * P * P)


def tile_conditionalvelocitymodel_b_kernel(
    tc, emb, cov, y_t, y_0_hat, wr1, br1, wr2, br2, wc, bc, wa, wb, wd, ua, ub, ud, offs, out
):
    nc = tc.nc
    cov_blocks = cov.rearrange("(k p) n -> p k n", p=P)
    with (
        tc.tile_pool(name="held", bufs=1) as held,
        tc.tile_pool(name="handed", bufs=LAG + 2) as handed,
        tc.tile_pool(name="rows", bufs=3) as rows,
        tc.tile_pool(name="work", bufs=3) as work,
        tc.psum_pool(name="psum_hid", bufs=2) as psum_hid,
        tc.psum_pool(name="psum_one", bufs=1) as psum_one,
    ):
        wr1_sb = held.tile([P, KC, HID], BF16, name="wr1_sb")
        nc.sync.dma_start(wr1_sb[:], wr1.rearrange("(k p) m -> p k m", p=P))
        br1_sb = [held.tile([P, 1], F32, name=f"br1_sb{h}") for h in range(KH)]
        for h in range(KH):
            nc.scalar.dma_start(br1_sb[h][:], br1[h * P : (h + 1) * P, :])
        wr2_sb = held.tile([P, KH, P], BF16, name="wr2_sb")
        nc.scalar.dma_start(wr2_sb[:], wr2.rearrange("(k p) m -> p k m", p=P))
        br2_sb = held.tile([P, 1], F32, name="br2_sb")
        nc.scalar.dma_start(br2_sb[:], br2)
        br2_scaled = held.tile([P, 1], F32, name="br2_scaled")
        nc.vector.tensor_scalar_add(br2_scaled[:], br2_sb[:], math.log(SPECIAL))
        ones_bf = held.tile([P, 1], BF16, name="ones_bf")
        nc.vector.memset(ones_bf[:], 1.0)

        cov_all = held.tile([P, KC, N], BF16, name="cov_all")

        def router(g):
            j0 = g * G
            cov_sb = cov_all[:, :, j0 : j0 + G]
            exp_z = work.tile([P, SPREAD, P], BF16, name="exp_z")
            exp_z_07 = handed.tile([P, G], F32, name="exp_z_07")
            for lo in range(0, G, T):
                nc.sync.dma_start(cov_sb[:, :, lo : lo + T], cov_blocks[:, :, j0 + lo : j0 + lo + T])
                hid_sb = work.tile([P, KH, T], BF16, name="hid_sb")
                for h in range(KH):
                    hid_ps = psum_hid.tile([P, T], F32, name="hid_ps")
                    for k in range(KC):
                        nc.tensor.matmul(
                            hid_ps[:],
                            wr1_sb[:, k, h * P : (h + 1) * P],
                            cov_sb[:, k, lo : lo + T],
                            start=(k == 0),
                            stop=(k == KC - 1),
                        )
                    nc.scalar.activation(hid_sb[:, h, :], hid_ps[:], ACT.Relu, bias=br1_sb[h][:])
                z_ps = psum_one.tile([P, T], F32, name="z_ps")
                for h in range(KH):
                    nc.tensor.matmul(
                        z_ps[:], wr2_sb[:, h, :], hid_sb[:, h, :], start=(h == 0), stop=(h == KH - 1)
                    )
                nc.scalar.activation(
                    exp_z[:, :, lo // SPREAD : (lo + T) // SPREAD],
                    z_ps[:].rearrange("e (m b) -> e b m", b=SPREAD),
                    ACT.Exp,
                    bias=br2_sb[:],
                )
                nc.scalar.activation(exp_z_07[:, lo : lo + T], z_ps[:], ACT.Exp, bias=br2_scaled[:])

            sums_ps = psum_one.tile([P, SPREAD], F32, name="sums_ps")
            for b in range(SPREAD):
                nc.tensor.matmul(sums_ps[:, b : b + 1], exp_z[:, b, :], ones_bf[:], start=True, stop=True)
            inv_sum = work.tile([P, SPREAD], F32, name="inv_sum")
            nc.vector.reciprocal(inv_sum[:], sums_ps[:])
            parked = out[P - 1 : P, j0 : j0 + G]
            nc.sync.dma_start(parked.rearrange("o (m b) -> (o m) b", b=SPREAD), inv_sum[:])
            inv_rows = handed.tile([P, G], F32, name="inv_rows")
            nc.sync.dma_start(inv_rows[:], parked.broadcast_to([P, G]))
            return cov_sb, exp_z_07, inv_rows

        rows_of = {}
        parts = {}

        def spot(t):
            g, lo = divmod(t * T, G)
            return g, slice(lo, lo + T)

        def weigh(t):
            g, cols = spot(t)
            if cols.start == 0:
                yt_sb = rows.tile([P, G], F32, name="yt_sb")
                nc.sync.dma_start(yt_sb[:], y_t[:, g * G : (g + 1) * G].broadcast_to([P, G]))
                y0_sb = rows.tile([P, G], F32, name="y0_sb")
                nc.sync.dma_start(y0_sb[:], y_0_hat[:, g * G : (g + 1) * G].broadcast_to([P, G]))
                rows_of[g] = (yt_sb, y0_sb)
            cov_sb, exp_z_07, inv_rows = routed[g]
            p_sb = work.tile([P, T], BF16, name="p_sb")
            nc.gpsimd.tensor_tensor(p_sb[:], exp_z_07[:, cols], inv_rows[:, cols], ALU.mult)
            parts[t] = {"p": p_sb}

        def share_a(t):
            g, cols = spot(t)
            a_ps = psum_one.tile([P, T], F32, name="a_ps")
            nc.tensor.matmul(a_ps[:], wa_sb[:], parts[t]["p"][:], start=True, stop=True)
            ma_yt = work.tile([P, T], F32, name="ma_yt")
            nc.vector.scalar_tensor_tensor(ma_yt[:], a_ps[:], ua_share[:], rows_of[g][0][:, cols], ALU.add, ALU.mult)
            parts[t]["ma_yt"] = ma_yt

        def share_b(t):
            g, cols = spot(t)
            b_ps = psum_one.tile([P, T], F32, name="b_ps")
            nc.tensor.matmul(b_ps[:], wb_sb[:], parts[t]["p"][:], start=True, stop=True)
            mb_y0 = work.tile([P, T], F32, name="mb_y0")
            nc.vector.scalar_tensor_tensor(mb_y0[:], b_ps[:], ub_share[:], rows_of[g][1][:, cols], ALU.add, ALU.mult)
            parts[t]["mb_y0"] = mb_y0

        def share_d(t):
            d_ps = psum_one.tile([P, T], F32, name="d_ps")
            nc.tensor.matmul(d_ps[:], wd_sb[:], parts[t]["p"][:], start=True, stop=True)
            md_more = work.tile([P, T], F32, name="md_more")
            nc.vector.scalar_tensor_tensor(md_more[:], d_ps[:], ud_share[:], parts[t]["ma_yt"][:], ALU.add, ALU.add)
            parts[t]["md_more"] = md_more

        def project(t):
            g, cols = spot(t)
            cov_sb = routed[g][0]
            mod_ps = psum_one.tile([P, T], F32, name="mod_ps")
            for k in range(KC):
                nc.tensor.matmul(
                    mod_ps[:], wc_sb[:, k, :], cov_sb[:, k, cols], start=(k == 0), stop=(k == KC - 1)
                )
            parts[t]["mod"] = mod_ps

        def add_up(t):
            mix = work.tile([P, T], F32, name="mix")
            nc.vector.tensor_tensor(mix[:], parts[t]["md_more"][:], parts[t]["mb_y0"][:], ALU.add)
            parts[t]["mix"] = mix

        def look_up(t):
            picked = emb_sb[:].indirect(offsets[:, t * T // 16 : (t + 1) * T // 16])
            q = work.tile([P, T], F32, name="q")
            nc.vector.tensor_tensor(q[:], picked, parts[t]["mix"][:], ALU.mult)
            parts[t]["q"] = q

        def modulate(t):
            v = v_all[:, t * T : (t + 1) * T]
            soft = soft_all[:, t * T : (t + 1) * T]
            nc.vector.scalar_tensor_tensor(v, parts[t]["mod"][:], bc_plus_1[:], parts[t]["q"][:], ALU.add, ALU.mult)
            nc.scalar.activation(soft, v, ACT.Abs)
            nc.scalar.activation(soft, soft, ACT.Exp, scale=-1.0)

        routed = [router(g) for g in range(LAG)]

        offsets = held.tile([P, N // 16], U16, name="offsets")
        nc.sync.dma_start(offsets[:], offs)
        wa_sb = held.tile([P, P], BF16, name="wa_sb")
        nc.sync.dma_start(wa_sb[:], wa)
        wb_sb = held.tile([P, P], BF16, name="wb_sb")
        nc.sync.dma_start(wb_sb[:], wb)
        wd_sb = held.tile([P, P], BF16, name="wd_sb")
        nc.sync.dma_start(wd_sb[:], wd)
        ua_sb = held.tile([P, 1], F32, name="ua_sb")
        nc.sync.dma_start(ua_sb[:], ua)
        ub_sb = held.tile([P, 1], F32, name="ub_sb")
        nc.sync.dma_start(ub_sb[:], ub)
        ud_sb = held.tile([P, 1], F32, name="ud_sb")
        nc.sync.dma_start(ud_sb[:], ud)
        emb_sb = held.tile([P, STEPS], F32, name="emb_sb")
        nc.sync.dma_start(emb_sb[:], emb)
        wc_sb = held.tile([P, KC, P], BF16, name="wc_sb")
        nc.sync.dma_start(wc_sb[:], wc.rearrange("(k p) m -> p k m", p=P))
        bc_sb = held.tile([P, 1], F32, name="bc_sb")
        nc.sync.dma_start(bc_sb[:], bc)
        ua_share = held.tile([P, 1], F32, name="ua_share")
        nc.vector.tensor_scalar_mul(ua_share[:], ua_sb[:], UNIVERSAL)
        ub_share = held.tile([P, 1], F32, name="ub_share")
        nc.vector.tensor_scalar_mul(ub_share[:], ub_sb[:], UNIVERSAL)
        ud_share = held.tile([P, 1], F32, name="ud_share")
        nc.vector.tensor_scalar_mul(ud_share[:], ud_sb[:], UNIVERSAL)
        bc_plus_1 = held.tile([P, 1], F32, name="bc_plus_1")
        nc.vector.tensor_scalar_add(bc_plus_1[:], bc_sb[:], 1.0)
        one_col = held.tile([P, 1], F32, name="one_col")
        nc.vector.memset(one_col[:], 1.0)

        v_all = held.tile([P, N], F32, name="v_all")
        soft_all = held.tile([P, N], F32, name="soft_all")
        routed.append(router(LAG))
        weigh(0)
        share_a(0)
        share_b(0)
        share_d(0)
        for first, tiles in zip((0, BATCHES[0] * G // T), (BATCHES[0] * G // T, BATCHES[1] * G // T)):
            for t in range(first, first + tiles):
                more = t + 1 < TILES
                g_next, cols_next = spot(t + 1)
                if cols_next.start == 0 and g_next + LAG < GROUPS:
                    routed.append(router(g_next + LAG))
                project(t)
                if more:
                    weigh(t + 1)
                    share_a(t + 1)
                add_up(t)
                if more:
                    share_b(t + 1)
                look_up(t)
                if more:
                    share_d(t + 1)
                modulate(t)
            batch = slice(first * T, (first + tiles) * T)
            nc.scalar.activation(soft_all[:, batch], soft_all[:, batch], ACT.Ln, bias=one_col[:])
        for at in range(0, N, T):
            nc.vector.scalar_tensor_tensor(
                soft_all[:, at : at + T], v_all[:, at : at + T], 0.0, soft_all[:, at : at + T], ALU.max, ALU.add
            )
            nc.sync.dma_start(out[:, at : at + T], soft_all[:, at : at + T])
